import numpy as np
import ml_dtypes


def mxq(x, axis, fmt="e4m3"):
    dtype, down = {"e4m3": (ml_dtypes.float8_e4m3fn, 7), "e5m2": (ml_dtypes.float8_e5m2, 14)}[fmt]
    v = np.moveaxis(np.asarray(x, np.float32).astype(ml_dtypes.bfloat16).astype(np.float64), axis, -1)
    blocks = v.reshape(v.shape[:-1] + (-1, 32))
    amax = np.abs(blocks).max(-1, keepdims=True)
    byte = np.maximum(np.where(amax > 0, np.frexp(amax)[1] - 1 + 127, 0) - down, 1)
    scale = np.exp2(byte - 127.0)
    codes = (blocks / scale).astype(np.float32).astype(dtype).astype(np.float64)
    return np.moveaxis((codes * scale).reshape(v.shape), -1, axis)


WIDE = False


def mx_kscale(k):
    if not WIDE:
        return np.ones(k)
    levels = np.array([10, -10, 5, -5, 0])
    a = np.random.permutation(np.resize(levels, k // 512 * 4)).reshape(k // 512, 4)
    idx = np.arange(k)
    return np.exp2(a[idx // 512, idx % 128 // 32])


BF16 = ml_dtypes.bfloat16


def bf(x):
    return np.asarray(x, np.float32).astype(BF16)


def f64(x):
    return np.asarray(x).astype(np.float64)


B, N, D, H, HD, FF = 2, 512, 1024, 8, 128, 4096
E = H * HD
EPS = 1e-5


def layernorm(x, gamma, beta):
    mu = x.mean(-1, keepdims=True)
    var = ((x - mu) ** 2).mean(-1, keepdims=True)
    return (x - mu) * (1.0 / np.sqrt(var + EPS)) * gamma + beta


def heads(y):
    return y.reshape(B, N, H, HD).transpose(0, 2, 1, 3)


def setup_inputs():
    s = mx_kscale(D)
    r = np.random.standard_normal
    return {"x": bf(r((B, N, D))),
            "gamma": bf((1.0 + 0.1 * r(D)) * s), "beta": bf(0.1 * r(D) * s),
            "Wq": bf(r((D, E)) * 1.4 / np.sqrt(D) / s[:, None]), "bq": bf(r(E) * 0.2),
            "Wk": bf(r((D, E)) * 1.4 / np.sqrt(D) / s[:, None]), "bk": bf(r(E) * 0.2),
            "Wv": bf(r((D, E)) * 1.0 / np.sqrt(D) / s[:, None]), "bv": bf(r(E) * 0.2)}


def reference(x, gamma, beta, Wq, bq, Wk, bk, Wv, bv):
    h = layernorm(f64(x), f64(gamma), f64(beta))
    hq = mxq(h, 2, "e4m3")
    q = (hq @ mxq(f64(Wq), 0, "e4m3")) + f64(bq)
    k = (hq @ mxq(f64(Wk), 0, "e4m3")) + f64(bk)
    v = (hq @ mxq(f64(Wv), 0, "e4m3")) + f64(bv)
    return heads(q), heads(k), heads(v)

@@ -1,0 +1,253 @@
+from contextlib import ExitStack
+
+import concourse.mybir as mybir
+from concourse.masks import make_identity
+
+F32 = mybir.dt.float32
+BF16 = mybir.dt.bfloat16
+U32 = mybir.dt.uint32
+U8 = mybir.dt.uint8
+I32 = mybir.dt.int32
+FP8X4 = mybir.dt.float8_e4m3fn_x4
+ACT = mybir.ActivationFunctionType
+ALU = mybir.AluOpType
+
+P = 128
+PACK = 4
+K_PASS = P * PACK
+
+BATCHES, ROWS, FEATURES, HEAD_DIM = 2, 512, 1024, 128
+OUT_COLS = 1024
+EPS = 1e-5
+
+PASSES = FEATURES // K_PASS
+ROW_TILES = ROWS // P
+BANK_COLS = 512
+COL_GROUPS = OUT_COLS // BANK_COLS
+GROUP_HEADS = BANK_COLS // HEAD_DIM
+STATS_CHUNK = 512
+STATS_CHUNKS = FEATURES // STATS_CHUNK
+RUN = 4
+
+FLOPS = 2 * BATCHES * ROWS * FEATURES * 3 * OUT_COLS
+
+
+def regroup(copy, grouped, rows):
+    copy(
+        out=grouped.rearrange("p (w r) j -> p w j r", r=RUN),
+        in_=rows.rearrange("p j (w r) -> p w j r", r=RUN),
+    )
+
+
+def tile_vit_transformerblock_pa_kernel(
+    tc, x, gamma, beta, Wq, bq, Wk, bk, Wv, bv, out_0, out_1, out_2
+):
+    nc = tc.nc
+    weights = (Wq, Wk, Wv)
+    biases = (bq, bk, bv)
+    outs = (out_0, out_1, out_2)
+
+    with ExitStack() as ctx:
+        const = ctx.enter_context(tc.tile_pool(name="const", bufs=1))
+        keep = ctx.enter_context(tc.tile_pool(name="keep", bufs=1))
+        small = ctx.enter_context(tc.tile_pool(name="small", bufs=2))
+        xhat_pool = ctx.enter_context(tc.tile_pool(name="xhat", bufs=2 * ROW_TILES))
+        plane_pool = ctx.enter_context(tc.tile_pool(name="planes", bufs=2))
+        group_pool = ctx.enter_context(tc.tile_pool(name="grouped", bufs=4))
+        out_pool = ctx.enter_context(tc.tile_pool(name="out", bufs=4))
+        flip_psum = ctx.enter_context(tc.psum_pool(name="flip", bufs=4))
+        sum_psum = ctx.enter_context(tc.psum_pool(name="sums", bufs=ROW_TILES))
+
+        x_rows = []
+        for b in range(BATCHES):
+            x_sb = keep.tile([P, ROW_TILES, FEATURES], BF16, name="x_sb_%d" % b)
+            by_row_tile = x[b].rearrange("(p i) d -> i p d", i=ROW_TILES)
+            for i in range(ROW_TILES):
+                nc.sync.dma_start(out=x_sb[:, i, :], in_=by_row_tile[i])
+            x_rows.append(x_sb)
+
+        w_rows = {}
+        for m in range(3):
+            for c in range(PASSES):
+                w_sb = keep.tile([P, PACK, OUT_COLS], BF16, name="w_sb_%d_%d" % (m, c))
+                nc.sync.dma_start(
+                    out=w_sb[:],
+                    in_=weights[m][c * K_PASS : (c + 1) * K_PASS, :].rearrange(
+                        "(p j) e -> p j e", j=PACK
+                    ),
+                )
+                w_rows[(m, c)] = w_sb
+
+        gamma_bf = const.tile([P, PASSES, PACK], BF16)
+        beta_bf = const.tile([P, PASSES, PACK], BF16)
+        nc.scalar.dma_start(
+            out=gamma_bf[:], in_=gamma.rearrange("(c p j) -> p c j", c=PASSES, j=PACK)
+        )
+        nc.scalar.dma_start(
+            out=beta_bf[:], in_=beta.rearrange("(c p j) -> p c j", c=PASSES, j=PACK)
+        )
+        bias_rows = const.tile([P, 3 * OUT_COLS], BF16)
+        nc.vector.memset(bias_rows[:].bitcast(I32), 0)
+        for m in range(3):
+            nc.scalar.dma_start(
+                out=bias_rows[0:1, m * OUT_COLS : (m + 1) * OUT_COLS],
+                in_=biases[m].rearrange("(o e) -> o e", o=1),
+            )
+
+        ident = const.tile([P, P], F32)
+        make_identity(nc, ident[:])
+        ones = const.tile([P, P], BF16)
+        nc.gpsimd.memset(ones[:], 1.0)
+        eps = const.tile([P, 1], F32)
+        nc.vector.memset(eps[:], EPS)
+        warm = const.tile([P, 1], F32)
+        nc.scalar.activation(out=warm[:], in_=eps[:], func=ACT.Sqrt)
+
+        gamma_f = const.tile([P, PASSES * PACK], F32)
+        beta_f = const.tile([P, PASSES * PACK], F32)
+        nc.vector.tensor_copy(out=gamma_f[:], in_=gamma_bf[:].rearrange("p c j -> p (c j)"))
+        nc.vector.tensor_copy(out=beta_f[:], in_=beta_bf[:].rearrange("p c j -> p (c j)"))
+
+        bias_all = const.tile([P, 3 * OUT_COLS], F32)
+        for s in range(3 * COL_GROUPS):
+            cols = slice(s * BANK_COLS, (s + 1) * BANK_COLS)
+            spread = flip_psum.tile([P, BANK_COLS], F32, tag="flip")
+            nc.tensor.matmul(out=spread[:], lhsT=ones[:], rhs=bias_rows[:, cols], start=True, stop=True)
+            nc.scalar.copy(out=bias_all[:, cols], in_=spread[:])
+
+        h_codes = [
+            keep.tile([P, PASSES, ROWS], U32, name="h_codes_%d" % b, align_bytes=64)
+            for b in range(BATCHES)
+        ]
+        h_scales = [
+            keep.tile([P, PASSES, ROWS], U8, name="h_scales_%d" % b, align_bytes=64)
+            for b in range(BATCHES)
+        ]
+        w_codes = [
+            keep.tile([P, PASSES, OUT_COLS], U32, name="w_codes_%d" % m, align_bytes=64)
+            for m in range(3)
+        ]
+        w_scales = [
+            keep.tile([P, PASSES, OUT_COLS], U8, name="w_scales_%d" % m, align_bytes=64)
+            for m in range(3)
+        ]
+
+        def quantise(codes, scales, grouped):
+            nc.vector.quantize_mx(
+                out=codes.bitcast(FP8X4),
+                scales=scales,
+                in_=grouped[:].rearrange("p w j -> p (w j)"),
+            )
+
+        def layer_norm(b):
+            x_sb = x_rows[b]
+
+            stats = small.tile([P, ROW_TILES, STATS_CHUNKS, 6], F32)
+            mean_var = small.tile([P, ROW_TILES, 2], F32)
+            for i in range(ROW_TILES):
+                for s in range(STATS_CHUNKS):
+                    nc.vector.bn_stats(
+                        out=stats[:, i, s, :],
+                        in_=x_sb[:, i, s * STATS_CHUNK : (s + 1) * STATS_CHUNK],
+                    )
+                nc.vector.bn_aggr(
+                    out=mean_var[:, i, :], in_=stats[:, i, :, :].rearrange("p s t -> p (s t)")
+                )
+            std = small.tile([P, ROW_TILES], F32)
+            nc.scalar.activation(out=std[:], in_=mean_var[:, :, 1], func=ACT.Sqrt, bias=eps[:, 0:1])
+            rstd = small.tile([P, ROW_TILES], F32)
+            nc.vector.reciprocal(out=rstd[:], in_=std[:])
+            shift = small.tile([P, ROW_TILES], F32)
+            nc.vector.scalar_tensor_tensor(
+                out=shift[:], in0=mean_var[:, :, 0], scalar=-1.0, in1=rstd[:],
+                op0=ALU.mult, op1=ALU.mult,
+            )
+
+            xhat_tiles = []
+            for i in range(ROW_TILES):
+                xhat = xhat_pool.tile([P, PASSES, PACK, P], F32)
+                every_fourth = x_sb[:, i, :].rearrange("p (c q j) -> p c j q", c=PASSES, j=PACK)
+                if i % 2 == 0:
+                    nc.scalar.activation(
+                        out=xhat[:],
+                        in_=every_fourth,
+                        func=ACT.Identity,
+                        scale=rstd[:, i : i + 1],
+                        bias=shift[:, i : i + 1],
+                    )
+                else:
+                    nc.gpsimd.tensor_scalar(
+                        out=xhat[:],
+                        in0=every_fourth,
+                        scalar1=rstd[:, i : i + 1],
+                        scalar2=shift[:, i : i + 1],
+                        op0=ALU.mult,
+                        op1=ALU.add,
+                    )
+                xhat_tiles.append(xhat)
+
+            for c in range(PASSES):
+                planes = plane_pool.tile([P, PACK, ROWS], BF16)
+                for j in range(PACK):
+                    flipped = flip_psum.tile([P, ROW_TILES, P], F32, tag="flip")
+                    for i in range(ROW_TILES):
+                        nc.tensor.transpose(flipped[:, i, :], xhat_tiles[i][:, c, j, :], ident[:])
+                    col = c * PACK + j
+                    nc.scalar.activation(
+                        out=planes[:, j, :],
+                        in_=flipped[:].rearrange("q i r -> q (i r)"),
+                        func=ACT.Identity,
+                        scale=gamma_f[:, col : col + 1],
+                        bias=beta_f[:, col : col + 1],
+                    )
+                grouped = group_pool.tile([P, BANK_COLS, PACK], BF16, align_bytes=64)
+                regroup(nc.vector.tensor_copy, grouped[:], planes[:])
+                quantise(h_codes[b][:, c, :], h_scales[b][:, c, :], grouped)
+
+        def quantise_weight(m, g):
+            cols = slice(g * BANK_COLS, (g + 1) * BANK_COLS)
+            for c in range(PASSES):
+                grouped = group_pool.tile([P, BANK_COLS, PACK], BF16, align_bytes=64)
+                regroup(nc.scalar.copy, grouped[:], w_rows[(m, c)][:, :, cols])
+                quantise(w_codes[m][:, c, cols], w_scales[m][:, c, cols], grouped)
+
+        def project(m, g, b):
+            cols = slice(g * BANK_COLS, (g + 1) * BANK_COLS)
+            bias_cols = bias_all[:, m * OUT_COLS + g * BANK_COLS : m * OUT_COLS + (g + 1) * BANK_COLS]
+            result = out_pool.tile([P, GROUP_HEADS, ROW_TILES, HEAD_DIM], F32)
+            for i in range(ROW_TILES):
+                rows = slice(i * P, (i + 1) * P)
+                sums = sum_psum.tile([P, BANK_COLS], F32)
+                for c in range(PASSES):
+                    nc.tensor.matmul_mx(
+                        out=sums[:],
+                        lhsT=h_codes[b][:, c, rows].bitcast(FP8X4),
+                        lhsT_scale=h_scales[b][:, c, rows],
+                        rhs=w_codes[m][:, c, cols].bitcast(FP8X4),
+                        rhs_scale=w_scales[m][:, c, cols],
+                        start=(c == 0),
+                        stop=(c == PASSES - 1),
+                    )
+                nc.vector.tensor_tensor(
+                    out=result[:, :, i, :],
+                    in0=sums[:].rearrange("p (a d) -> p a d", a=GROUP_HEADS),
+                    in1=bias_cols.rearrange("p (a d) -> p a d", a=GROUP_HEADS),
+                    op=ALU.add,
+                )
+            nc.sync.dma_start(
+                out=outs[m][b, g * GROUP_HEADS : (g + 1) * GROUP_HEADS].rearrange(
+                    "a (p i) d -> p a (i d)", i=ROW_TILES
+                ),
+                in_=result[:].rearrange("p a i d -> p a (i d)"),
+            )
+
+        for m in range(3):
+            for g in range(COL_GROUPS):
+                first = m == 0 and g == 0
+                if first:
+                    layer_norm(0)
+                quantise_weight(m, g)
+                project(m, g, 0)
+                if first:
+                    layer_norm(1)
+                project(m, g, 1)

@@ -28,6 +28,8 @@ GROUP_HEADS = BANK_COLS // HEAD_DIM
 STATS_CHUNK = 512
 STATS_CHUNKS = FEATURES // STATS_CHUNK
 RUN = 4
+AHEAD = 3
+STORE_TILES = 2
 
 FLOPS = 2 * BATCHES * ROWS * FEATURES * 3 * OUT_COLS
 
@@ -50,13 +52,13 @@ def tile_vit_transformerblock_pa_kernel(
     with ExitStack() as ctx:
         const = ctx.enter_context(tc.tile_pool(name="const", bufs=1))
         keep = ctx.enter_context(tc.tile_pool(name="keep", bufs=1))
-        small = ctx.enter_context(tc.tile_pool(name="small", bufs=2))
-        xhat_pool = ctx.enter_context(tc.tile_pool(name="xhat", bufs=2 * ROW_TILES))
+        xhat_pool = ctx.enter_context(tc.tile_pool(name="xhat", bufs=BATCHES * ROW_TILES))
         plane_pool = ctx.enter_context(tc.tile_pool(name="planes", bufs=2))
         group_pool = ctx.enter_context(tc.tile_pool(name="grouped", bufs=4))
         out_pool = ctx.enter_context(tc.tile_pool(name="out", bufs=4))
         flip_psum = ctx.enter_context(tc.psum_pool(name="flip", bufs=4))
         sum_psum = ctx.enter_context(tc.psum_pool(name="sums", bufs=ROW_TILES))
+        ctx.enter_context(tc.manual_schedule())
 
         x_rows = []
         for b in range(BATCHES):
@@ -102,18 +104,10 @@ def tile_vit_transformerblock_pa_kernel(
         nc.vector.memset(eps[:], EPS)
         warm = const.tile([P, 1], F32)
         nc.scalar.activation(out=warm[:], in_=eps[:], func=ACT.Sqrt)
-
         gamma_f = const.tile([P, PASSES * PACK], F32)
         beta_f = const.tile([P, PASSES * PACK], F32)
-        nc.vector.tensor_copy(out=gamma_f[:], in_=gamma_bf[:].rearrange("p c j -> p (c j)"))
-        nc.vector.tensor_copy(out=beta_f[:], in_=beta_bf[:].rearrange("p c j -> p (c j)"))
-
-        bias_all = const.tile([P, 3 * OUT_COLS], F32)
-        for s in range(3 * COL_GROUPS):
-            cols = slice(s * BANK_COLS, (s + 1) * BANK_COLS)
-            spread = flip_psum.tile([P, BANK_COLS], F32, tag="flip")
-            nc.tensor.matmul(out=spread[:], lhsT=ones[:], rhs=bias_rows[:, cols], start=True, stop=True)
-            nc.scalar.copy(out=bias_all[:, cols], in_=spread[:])
+        nc.scalar.copy(out=gamma_f[:], in_=gamma_bf[:].rearrange("p c j -> p (c j)"))
+        nc.scalar.copy(out=beta_f[:], in_=beta_bf[:].rearrange("p c j -> p (c j)"))
 
         h_codes = [
             keep.tile([P, PASSES, ROWS], U32, name="h_codes_%d" % b, align_bytes=64)
@@ -131,6 +125,7 @@ def tile_vit_transformerblock_pa_kernel(
             keep.tile([P, PASSES, OUT_COLS], U8, name="w_scales_%d" % m, align_bytes=64)
             for m in range(3)
         ]
+        bias_all = const.tile([P, 3 * OUT_COLS], F32)
 
         def quantise(codes, scales, grouped):
             nc.vector.quantize_mx(
@@ -139,79 +134,101 @@ def tile_vit_transformerblock_pa_kernel(
                 in_=grouped[:].rearrange("p w j -> p (w j)"),
             )
 
-        def layer_norm(b):
-            x_sb = x_rows[b]
+        row_tiles = [(b, i) for b in range(BATCHES) for i in range(ROW_TILES)]
+        stats = const.tile([P, len(row_tiles), STATS_CHUNKS, 6], F32)
+        mean_var = const.tile([P, len(row_tiles), 2], F32)
+        std = const.tile([P, len(row_tiles)], F32)
+        rstd = const.tile([P, len(row_tiles)], F32)
+        shift = const.tile([P, len(row_tiles)], F32)
+        xhat_tiles = {}
 
-            stats = small.tile([P, ROW_TILES, STATS_CHUNKS, 6], F32)
-            mean_var = small.tile([P, ROW_TILES, 2], F32)
-            for i in range(ROW_TILES):
-                for s in range(STATS_CHUNKS):
-                    nc.vector.bn_stats(
-                        out=stats[:, i, s, :],
-                        in_=x_sb[:, i, s * STATS_CHUNK : (s + 1) * STATS_CHUNK],
-                    )
-                nc.vector.bn_aggr(
-                    out=mean_var[:, i, :], in_=stats[:, i, :, :].rearrange("p s t -> p (s t)")
+        def deviation(t):
+            b, i = row_tiles[t]
+            for s in range(STATS_CHUNKS):
+                nc.vector.bn_stats(
+                    out=stats[:, t, s, :],
+                    in_=x_rows[b][:, i, s * STATS_CHUNK : (s + 1) * STATS_CHUNK],
                 )
-            std = small.tile([P, ROW_TILES], F32)
-            nc.scalar.activation(out=std[:], in_=mean_var[:, :, 1], func=ACT.Sqrt, bias=eps[:, 0:1])
-            rstd = small.tile([P, ROW_TILES], F32)
-            nc.vector.reciprocal(out=rstd[:], in_=std[:])
-            shift = small.tile([P, ROW_TILES], F32)
-            nc.vector.scalar_tensor_tensor(
-                out=shift[:], in0=mean_var[:, :, 0], scalar=-1.0, in1=rstd[:],
-                op0=ALU.mult, op1=ALU.mult,
+            nc.vector.bn_aggr(
+                out=mean_var[:, t, :], in_=stats[:, t, :, :].rearrange("p s u -> p (s u)")
+            )
+            nc.scalar.activation(
+                out=std[:, t : t + 1], in_=mean_var[:, t, 1:2], func=ACT.Sqrt, bias=eps[:, 0:1]
             )
 
-            xhat_tiles = []
-            for i in range(ROW_TILES):
-                xhat = xhat_pool.tile([P, PASSES, PACK, P], F32)
-                every_fourth = x_sb[:, i, :].rearrange("p (c q j) -> p c j q", c=PASSES, j=PACK)
-                if i % 2 == 0:
-                    nc.scalar.activation(
-                        out=xhat[:],
-                        in_=every_fourth,
-                        func=ACT.Identity,
-                        scale=rstd[:, i : i + 1],
-                        bias=shift[:, i : i + 1],
-                    )
-                else:
-                    nc.gpsimd.tensor_scalar(
-                        out=xhat[:],
-                        in0=every_fourth,
-                        scalar1=rstd[:, i : i + 1],
-                        scalar2=shift[:, i : i + 1],
-                        op0=ALU.mult,
-                        op1=ALU.add,
-                    )
-                xhat_tiles.append(xhat)
+        def normalise(t):
+            b, i = row_tiles[t]
+            nc.vector.reciprocal(out=rstd[:, t : t + 1], in_=std[:, t : t + 1])
+            nc.vector.scalar_tensor_tensor(
+                out=shift[:, t : t + 1], in0=mean_var[:, t, 0:1], scalar=-1.0, in1=rstd[:, t : t + 1],
+                op0=ALU.mult, op1=ALU.mult,
+            )
+            xhat = xhat_pool.tile([P, PASSES, PACK, P], F32)
+            nc.gpsimd.tensor_scalar(
+                out=xhat[:],
+                in0=x_rows[b][:, i, :].rearrange("p (c q j) -> p c j q", c=PASSES, j=PACK),
+                scalar1=rstd[:, t : t + 1],
+                scalar2=shift[:, t : t + 1],
+                op0=ALU.mult,
+                op1=ALU.add,
+            )
+            xhat_tiles[(b, i)] = xhat
 
+        for t in range(len(row_tiles)):
+            deviation(t)
+            if t > 0:
+                normalise(t - 1)
+        normalise(len(row_tiles) - 1)
+
+        def transpose_scale(b, c):
+            planes = plane_pool.tile([P, PACK, ROWS], BF16)
+            for j in range(PACK):
+                flipped = flip_psum.tile([P, ROW_TILES, P], F32, tag="flip")
+                for i in range(ROW_TILES):
+                    nc.tensor.transpose(flipped[:, i, :], xhat_tiles[(b, i)][:, c, j, :], ident[:])
+                col = c * PACK + j
+                nc.scalar.activation(
+                    out=planes[:, j, :],
+                    in_=flipped[:].rearrange("q i r -> q (i r)"),
+                    func=ACT.Identity,
+                    scale=gamma_f[:, col : col + 1],
+                    bias=beta_f[:, col : col + 1],
+                )
+            return planes
+
+        def pack_h(b, planes_of_pass):
+            grouped_of_pass = []
             for c in range(PASSES):
-                planes = plane_pool.tile([P, PACK, ROWS], BF16)
-                for j in range(PACK):
-                    flipped = flip_psum.tile([P, ROW_TILES, P], F32, tag="flip")
-                    for i in range(ROW_TILES):
-                        nc.tensor.transpose(flipped[:, i, :], xhat_tiles[i][:, c, j, :], ident[:])
-                    col = c * PACK + j
-                    nc.scalar.activation(
-                        out=planes[:, j, :],
-                        in_=flipped[:].rearrange("q i r -> q (i r)"),
-                        func=ACT.Identity,
-                        scale=gamma_f[:, col : col + 1],
-                        bias=beta_f[:, col : col + 1],
-                    )
                 grouped = group_pool.tile([P, BANK_COLS, PACK], BF16, align_bytes=64)
-                regroup(nc.vector.tensor_copy, grouped[:], planes[:])
-                quantise(h_codes[b][:, c, :], h_scales[b][:, c, :], grouped)
+                regroup(nc.vector.tensor_copy, grouped[:], planes_of_pass[c][:])
+                grouped_of_pass.append(grouped)
+            for c in range(PASSES):
+                quantise(h_codes[b][:, c, :], h_scales[b][:, c, :], grouped_of_pass[c])
 
-        def quantise_weight(m, g):
+        quarters = [
+            (m, g, c) for m in range(3) for g in range(COL_GROUPS) for c in range(PASSES)
+        ]
+
+        def quantise_quarter(n, copy):
+            m, g, c = quarters[n]
             cols = slice(g * BANK_COLS, (g + 1) * BANK_COLS)
-            for c in range(PASSES):
-                grouped = group_pool.tile([P, BANK_COLS, PACK], BF16, align_bytes=64)
-                regroup(nc.scalar.copy, grouped[:], w_rows[(m, c)][:, :, cols])
-                quantise(w_codes[m][:, c, cols], w_scales[m][:, c, cols], grouped)
+            grouped = group_pool.tile([P, BANK_COLS, PACK], BF16, align_bytes=64)
+            regroup(copy, grouped[:], w_rows[(m, c)][:, :, cols])
+            quantise(w_codes[m][:, c, cols], w_scales[m][:, c, cols], grouped)
+            if c == PASSES - 1:
+                bias_cols = slice(m * OUT_COLS + g * BANK_COLS, m * OUT_COLS + (g + 1) * BANK_COLS)
+                spread = flip_psum.tile([P, BANK_COLS], F32, tag="flip")
+                nc.tensor.matmul(
+                    out=spread[:], lhsT=ones[:], rhs=bias_rows[:, bias_cols], start=True, stop=True
+                )
+                nc.scalar.copy(out=bias_all[:, bias_cols], in_=spread[:])
 
-        def project(m, g, b):
+        products = [
+            (m, g, b) for m in range(3) for g in range(COL_GROUPS) for b in range(BATCHES)
+        ]
+
+        def project(n):
+            m, g, b = products[n]
             cols = slice(g * BANK_COLS, (g + 1) * BANK_COLS)
             bias_cols = bias_all[:, m * OUT_COLS + g * BANK_COLS : m * OUT_COLS + (g + 1) * BANK_COLS]
             result = out_pool.tile([P, GROUP_HEADS, ROW_TILES, HEAD_DIM], F32)
@@ -234,20 +251,25 @@ def tile_vit_transformerblock_pa_kernel(
                     in1=bias_cols.rearrange("p (a d) -> p a d", a=GROUP_HEADS),
                     op=ALU.add,
                 )
-            nc.sync.dma_start(
-                out=outs[m][b, g * GROUP_HEADS : (g + 1) * GROUP_HEADS].rearrange(
-                    "a (p i) d -> p a (i d)", i=ROW_TILES
-                ),
-                in_=result[:].rearrange("p a i d -> p a (i d)"),
-            )
+                if (i + 1) % STORE_TILES == 0:
+                    done = slice(i + 1 - STORE_TILES, i + 1)
+                    nc.sync.dma_start(
+                        out=outs[m][b, g * GROUP_HEADS : (g + 1) * GROUP_HEADS].rearrange(
+                            "a (p i) d -> p a i d", i=ROW_TILES
+                        )[:, :, done, :],
+                        in_=result[:, :, done, :],
+                    )
 
-        for m in range(3):
-            for g in range(COL_GROUPS):
-                first = m == 0 and g == 0
-                if first:
-                    layer_norm(0)
-                quantise_weight(m, g)
-                project(m, g, 0)
-                if first:
-                    layer_norm(1)
-                project(m, g, 1)
+        quantise_quarter(0, nc.vector.tensor_copy)
+        quantise_quarter(1, nc.vector.tensor_copy)
+        pack_h(0, [transpose_scale(0, c) for c in range(PASSES)])
+        planes_1 = [transpose_scale(1, 0)]
+        project(0)
+        quantise_quarter(2, nc.scalar.copy)
+        planes_1.append(transpose_scale(1, 1))
+        pack_h(1, planes_1)
+        quantise_quarter(3, nc.scalar.copy)
+        for n in range(1, len(products)):
+            project(n)
+            if n + AHEAD < len(quarters):
+                quantise_quarter(n + AHEAD, nc.scalar.copy)

@@ -29,7 +29,8 @@ STATS_CHUNK = 512
 STATS_CHUNKS = FEATURES // STATS_CHUNK
 RUN = 4
 AHEAD = 3
-STORE_TILES = 2
+STORE_TILES = 4
+LAST_STORE_TILES = 2
 
 FLOPS = 2 * BATCHES * ROWS * FEATURES * 3 * OUT_COLS
 
@@ -251,8 +252,9 @@ def tile_vit_transformerblock_pa_kernel(
                     in1=bias_cols.rearrange("p (a d) -> p a d", a=GROUP_HEADS),
                     op=ALU.add,
                 )
-                if (i + 1) % STORE_TILES == 0:
-                    done = slice(i + 1 - STORE_TILES, i + 1)
+                step = LAST_STORE_TILES if n == len(products) - 1 else STORE_TILES
+                if (i + 1) % step == 0:
+                    done = slice(i + 1 - step, i + 1)
                     nc.sync.dma_start(
                         out=outs[m][b, g * GROUP_HEADS : (g + 1) * GROUP_HEADS].rearrange(
                             "a (p i) d -> p a i d", i=ROW_TILES

@@ -29,8 +29,7 @@ STATS_CHUNK = 512
 STATS_CHUNKS = FEATURES // STATS_CHUNK
 RUN = 4
 AHEAD = 3
-STORE_TILES = 4
-LAST_STORE_TILES = 2
+STORE_TILES = 2
 
 FLOPS = 2 * BATCHES * ROWS * FEATURES * 3 * OUT_COLS
 
@@ -54,7 +53,7 @@ def tile_vit_transformerblock_pa_kernel(
         const = ctx.enter_context(tc.tile_pool(name="const", bufs=1))
         keep = ctx.enter_context(tc.tile_pool(name="keep", bufs=1))
         xhat_pool = ctx.enter_context(tc.tile_pool(name="xhat", bufs=BATCHES * ROW_TILES))
-        plane_pool = ctx.enter_context(tc.tile_pool(name="planes", bufs=2))
+        plane_pool = ctx.enter_context(tc.tile_pool(name="planes", bufs=4))
         group_pool = ctx.enter_context(tc.tile_pool(name="grouped", bufs=4))
         out_pool = ctx.enter_context(tc.tile_pool(name="out", bufs=4))
         flip_psum = ctx.enter_context(tc.psum_pool(name="flip", bufs=4))
@@ -90,7 +89,7 @@ def tile_vit_transformerblock_pa_kernel(
             out=beta_bf[:], in_=beta.rearrange("(c p j) -> p c j", c=PASSES, j=PACK)
         )
         bias_rows = const.tile([P, 3 * OUT_COLS], BF16)
-        nc.vector.memset(bias_rows[:].bitcast(I32), 0)
+        nc.gpsimd.memset(bias_rows[:], 0.0)
         for m in range(3):
             nc.scalar.dma_start(
                 out=bias_rows[0:1, m * OUT_COLS : (m + 1) * OUT_COLS],
@@ -135,6 +134,7 @@ def tile_vit_transformerblock_pa_kernel(
                 in_=grouped[:].rearrange("p w j -> p (w j)"),
             )
 
+
         row_tiles = [(b, i) for b in range(BATCHES) for i in range(ROW_TILES)]
         stats = const.tile([P, len(row_tiles), STATS_CHUNKS, 6], F32)
         mean_var = const.tile([P, len(row_tiles), 2], F32)
@@ -142,136 +142,178 @@ def tile_vit_transformerblock_pa_kernel(
         rstd = const.tile([P, len(row_tiles)], F32)
         shift = const.tile([P, len(row_tiles)], F32)
         xhat_tiles = {}
+        planes = {}
+        grouped_h = {}
+        grouped_w = {}
+        flips = {}
+        sums_of = {}
+        results = {}
 
-        def deviation(t):
+        def bs(t, s):
             b, i = row_tiles[t]
-            for s in range(STATS_CHUNKS):
-                nc.vector.bn_stats(
-                    out=stats[:, t, s, :],
-                    in_=x_rows[b][:, i, s * STATS_CHUNK : (s + 1) * STATS_CHUNK],
-                )
-            nc.vector.bn_aggr(
-                out=mean_var[:, t, :], in_=stats[:, t, :, :].rearrange("p s u -> p (s u)")
-            )
-            nc.scalar.activation(
-                out=std[:, t : t + 1], in_=mean_var[:, t, 1:2], func=ACT.Sqrt, bias=eps[:, 0:1]
-            )
+            nc.vector.bn_stats(out=stats[:, t, s, :], in_=x_rows[b][:, i, s * STATS_CHUNK : (s + 1) * STATS_CHUNK])
 
-        def normalise(t):
-            b, i = row_tiles[t]
+        def aggr(t):
+            nc.vector.bn_aggr(out=mean_var[:, t, :], in_=stats[:, t, :, :].rearrange("p s u -> p (s u)"))
+            nc.scalar.activation(out=std[:, t : t + 1], in_=mean_var[:, t, 1:2], func=ACT.Sqrt, bias=eps[:, 0:1])
+
+        def small(t):
             nc.vector.reciprocal(out=rstd[:, t : t + 1], in_=std[:, t : t + 1])
             nc.vector.scalar_tensor_tensor(
                 out=shift[:, t : t + 1], in0=mean_var[:, t, 0:1], scalar=-1.0, in1=rstd[:, t : t + 1],
                 op0=ALU.mult, op1=ALU.mult,
             )
-            xhat = xhat_pool.tile([P, PASSES, PACK, P], F32)
-            nc.gpsimd.tensor_scalar(
-                out=xhat[:],
-                in0=x_rows[b][:, i, :].rearrange("p (c q j) -> p c j q", c=PASSES, j=PACK),
-                scalar1=rstd[:, t : t + 1],
-                scalar2=shift[:, t : t + 1],
-                op0=ALU.mult,
-                op1=ALU.add,
-            )
+
+        def xhat_of(t, eng):
+            b, i = row_tiles[t]
+            xhat = xhat_pool.tile([P, PASSES, PACK, P], F32, name="xhat")
+            src = x_rows[b][:, i, :].rearrange("p (c q j) -> p c j q", c=PASSES, j=PACK)
+            if eng == "G":
+                nc.gpsimd.tensor_scalar(out=xhat[:], in0=src, scalar1=rstd[:, t : t + 1], scalar2=shift[:, t : t + 1], op0=ALU.mult, op1=ALU.add)
+            elif eng == "V":
+                nc.vector.tensor_scalar(out=xhat[:], in0=src, scalar1=rstd[:, t : t + 1], scalar2=shift[:, t : t + 1], op0=ALU.mult, op1=ALU.add)
+            else:
+                nc.scalar.activation(out=xhat[:], in_=src, func=ACT.Identity, scale=rstd[:, t : t + 1], bias=shift[:, t : t + 1])
             xhat_tiles[(b, i)] = xhat
 
-        for t in range(len(row_tiles)):
-            deviation(t)
-            if t > 0:
-                normalise(t - 1)
-        normalise(len(row_tiles) - 1)
+        def flip(b, c, j):
+            flipped = flip_psum.tile([P, ROW_TILES, P], F32, tag="flip")
+            for i in range(ROW_TILES):
+                nc.tensor.transpose(flipped[:, i, :], xhat_tiles[(b, i)][:, c, j, :], ident[:])
+            flips[(b, c, j)] = flipped
 
-        def transpose_scale(b, c):
-            planes = plane_pool.tile([P, PACK, ROWS], BF16)
-            for j in range(PACK):
-                flipped = flip_psum.tile([P, ROW_TILES, P], F32, tag="flip")
-                for i in range(ROW_TILES):
-                    nc.tensor.transpose(flipped[:, i, :], xhat_tiles[(b, i)][:, c, j, :], ident[:])
-                col = c * PACK + j
-                nc.scalar.activation(
-                    out=planes[:, j, :],
-                    in_=flipped[:].rearrange("q i r -> q (i r)"),
-                    func=ACT.Identity,
-                    scale=gamma_f[:, col : col + 1],
-                    bias=beta_f[:, col : col + 1],
-                )
-            return planes
+        def exit_h(b, c, j, eng):
+            if j == 0:
+                planes[(b, c)] = plane_pool.tile([P, PACK, ROWS], BF16, name="planes")
+            col = c * PACK + j
+            src = flips[(b, c, j)][:].rearrange("q i r -> q (i r)")
+            if eng == "S":
+                nc.scalar.activation(out=planes[(b, c)][:, j, :], in_=src, func=ACT.Identity, scale=gamma_f[:, col : col + 1], bias=beta_f[:, col : col + 1])
+            else:
+                nc.vector.tensor_scalar(out=planes[(b, c)][:, j, :], in0=src, scalar1=gamma_f[:, col : col + 1], scalar2=beta_f[:, col : col + 1], op0=ALU.mult, op1=ALU.add)
 
-        def pack_h(b, planes_of_pass):
-            grouped_of_pass = []
-            for c in range(PASSES):
-                grouped = group_pool.tile([P, BANK_COLS, PACK], BF16, align_bytes=64)
-                regroup(nc.vector.tensor_copy, grouped[:], planes_of_pass[c][:])
-                grouped_of_pass.append(grouped)
-            for c in range(PASSES):
-                quantise(h_codes[b][:, c, :], h_scales[b][:, c, :], grouped_of_pass[c])
+        def gp_copy(out, in_):
+            nc.gpsimd.tensor_scalar(out=out, in0=in_, scalar1=1.0, scalar2=0.0, op0=ALU.mult, op1=ALU.add)
 
-        quarters = [
-            (m, g, c) for m in range(3) for g in range(COL_GROUPS) for c in range(PASSES)
-        ]
+        COPY = {"V": nc.vector.tensor_copy, "S": nc.scalar.copy, "G": gp_copy}
 
-        def quantise_quarter(n, copy):
+        def hreg(b, c, eng, pieces=1):
+            grouped = group_pool.tile([P, BANK_COLS, PACK], BF16, align_bytes=64, name="grouped")
+            w = BANK_COLS // pieces
+            for k in range(pieces):
+                regroup(COPY[eng], grouped[:, k * w : (k + 1) * w, :], planes[(b, c)][:, :, k * w : (k + 1) * w])
+            grouped_h[(b, c)] = grouped
+
+        def hquant(b, c):
+            quantise(h_codes[b][:, c, :], h_scales[b][:, c, :], grouped_h[(b, c)])
+
+        quarters = [(m, g, c) for m in range(3) for g in range(COL_GROUPS) for c in range(PASSES)]
+
+        def wreg(n, eng, lo=0, hi=BANK_COLS):
+            m, g, c = quarters[n]
+            if lo == 0:
+                grouped_w[n] = group_pool.tile([P, BANK_COLS, PACK], BF16, align_bytes=64, name="grouped")
+            regroup(COPY[eng], grouped_w[n][:, lo:hi, :], w_rows[(m, c)][:, :, g * BANK_COLS + lo : g * BANK_COLS + hi])
+
+        def wquant(n):
             m, g, c = quarters[n]
             cols = slice(g * BANK_COLS, (g + 1) * BANK_COLS)
-            grouped = group_pool.tile([P, BANK_COLS, PACK], BF16, align_bytes=64)
-            regroup(copy, grouped[:], w_rows[(m, c)][:, :, cols])
-            quantise(w_codes[m][:, c, cols], w_scales[m][:, c, cols], grouped)
-            if c == PASSES - 1:
-                bias_cols = slice(m * OUT_COLS + g * BANK_COLS, m * OUT_COLS + (g + 1) * BANK_COLS)
-                spread = flip_psum.tile([P, BANK_COLS], F32, tag="flip")
-                nc.tensor.matmul(
-                    out=spread[:], lhsT=ones[:], rhs=bias_rows[:, bias_cols], start=True, stop=True
-                )
-                nc.scalar.copy(out=bias_all[:, bias_cols], in_=spread[:])
+            quantise(w_codes[m][:, c, cols], w_scales[m][:, c, cols], grouped_w[n])
 
-        products = [
-            (m, g, b) for m in range(3) for g in range(COL_GROUPS) for b in range(BATCHES)
-        ]
+        def spread(m, g):
+            bias_cols = slice(m * OUT_COLS + g * BANK_COLS, m * OUT_COLS + (g + 1) * BANK_COLS)
+            sp = flip_psum.tile([P, BANK_COLS], F32, tag="flip")
+            nc.tensor.matmul(out=sp[:], lhsT=ones[:], rhs=bias_rows[:, bias_cols], start=True, stop=True)
+            nc.scalar.copy(out=bias_all[:, bias_cols], in_=sp[:])
 
-        def project(n):
+        products = [(m, g, b) for m in range(3) for g in range(COL_GROUPS) for b in range(BATCHES)]
+
+        def mm(n, i):
             m, g, b = products[n]
             cols = slice(g * BANK_COLS, (g + 1) * BANK_COLS)
-            bias_cols = bias_all[:, m * OUT_COLS + g * BANK_COLS : m * OUT_COLS + (g + 1) * BANK_COLS]
-            result = out_pool.tile([P, GROUP_HEADS, ROW_TILES, HEAD_DIM], F32)
-            for i in range(ROW_TILES):
-                rows = slice(i * P, (i + 1) * P)
-                sums = sum_psum.tile([P, BANK_COLS], F32)
-                for c in range(PASSES):
-                    nc.tensor.matmul_mx(
-                        out=sums[:],
-                        lhsT=h_codes[b][:, c, rows].bitcast(FP8X4),
-                        lhsT_scale=h_scales[b][:, c, rows],
-                        rhs=w_codes[m][:, c, cols].bitcast(FP8X4),
-                        rhs_scale=w_scales[m][:, c, cols],
-                        start=(c == 0),
-                        stop=(c == PASSES - 1),
-                    )
-                nc.vector.tensor_tensor(
-                    out=result[:, :, i, :],
-                    in0=sums[:].rearrange("p (a d) -> p a d", a=GROUP_HEADS),
-                    in1=bias_cols.rearrange("p (a d) -> p a d", a=GROUP_HEADS),
-                    op=ALU.add,
+            rows = slice(i * P, (i + 1) * P)
+            sums = sum_psum.tile([P, BANK_COLS], F32, name="sums")
+            for c in range(PASSES):
+                nc.tensor.matmul_mx(
+                    out=sums[:], lhsT=h_codes[b][:, c, rows].bitcast(FP8X4), lhsT_scale=h_scales[b][:, c, rows],
+                    rhs=w_codes[m][:, c, cols].bitcast(FP8X4), rhs_scale=w_scales[m][:, c, cols],
+                    start=(c == 0), stop=(c == PASSES - 1),
                 )
-                step = LAST_STORE_TILES if n == len(products) - 1 else STORE_TILES
-                if (i + 1) % step == 0:
-                    done = slice(i + 1 - step, i + 1)
-                    nc.sync.dma_start(
-                        out=outs[m][b, g * GROUP_HEADS : (g + 1) * GROUP_HEADS].rearrange(
-                            "a (p i) d -> p a i d", i=ROW_TILES
-                        )[:, :, done, :],
-                        in_=result[:, :, done, :],
-                    )
+            sums_of[(n, i)] = sums
 
-        quantise_quarter(0, nc.vector.tensor_copy)
-        quantise_quarter(1, nc.vector.tensor_copy)
-        pack_h(0, [transpose_scale(0, c) for c in range(PASSES)])
-        planes_1 = [transpose_scale(1, 0)]
-        project(0)
-        quantise_quarter(2, nc.scalar.copy)
-        planes_1.append(transpose_scale(1, 1))
-        pack_h(1, planes_1)
-        quantise_quarter(3, nc.scalar.copy)
+        def add(n, i):
+            m, g, b = products[n]
+            if i == 0:
+                results[n] = out_pool.tile([P, GROUP_HEADS, ROW_TILES, HEAD_DIM], F32, name="result")
+            bias_cols = bias_all[:, m * OUT_COLS + g * BANK_COLS : m * OUT_COLS + (g + 1) * BANK_COLS]
+            nc.vector.tensor_tensor(
+                out=results[n][:, :, i, :], in0=sums_of[(n, i)][:].rearrange("p (a d) -> p a d", a=GROUP_HEADS),
+                in1=bias_cols.rearrange("p (a d) -> p a d", a=GROUP_HEADS), op=ALU.add,
+            )
+
+        def store(n, lo, hi):
+            m, g, b = products[n]
+            nc.sync.dma_start(
+                out=outs[m][b, g * GROUP_HEADS : (g + 1) * GROUP_HEADS].rearrange("a (p i) d -> p a i d", i=ROW_TILES)[:, :, lo:hi, :],
+                in_=results[n][:, :, lo:hi, :],
+            )
+
+        def project(n, st=STORE_TILES):
+            for i in range(ROW_TILES):
+                mm(n, i)
+                add(n, i)
+                if (i + 1) % st == 0:
+                    store(n, i + 1 - st, i + 1)
+
+        for t in range(8):
+            bs(t, 0)
+            if t > 0:
+                small(t - 1)
+                xhat_of(t - 1, "G")
+            bs(t, 1)
+            aggr(t)
+            if t == 4:
+                wreg(0, "S", 0, 256)
+            if t == 5:
+                wreg(0, "S", 256, 512)
+            if t == 6:
+                for j in range(2):
+                    flip(0, 0, j)
+                    exit_h(0, 0, j, "S")
+        small(7)
+        xhat_of(7, "G")
+        for j in range(2, 4):
+            flip(0, 0, j)
+            exit_h(0, 0, j, "S")
+        for j in range(4):
+            flip(0, 1, j)
+            exit_h(0, 1, j, "V")
+        wreg(1, "S")
+        spread(0, 0)
+        hreg(0, 0, "V")
+        hreg(0, 1, "V")
+        wquant(0)
+        hquant(0, 0)
+        hquant(0, 1)
+        wquant(1)
+        for c in range(2):
+            for j in range(4):
+                flip(1, c, j)
+                exit_h(1, c, j, "S")
+        project(0, ROW_TILES)
+        hreg(1, 0, "V")
+        hreg(1, 1, "V")
+        wreg(2, "S")
+        hquant(1, 0)
+        hquant(1, 1)
+        wquant(2)
+        wreg(3, "S")
+        wquant(3)
+        spread(0, 1)
         for n in range(1, len(products)):
-            project(n)
+            project(n, ROW_TILES if n < len(products) - 1 else STORE_TILES)
             if n + AHEAD < len(quarters):
-                quantise_quarter(n + AHEAD, nc.scalar.copy)
+                wreg(n + AHEAD, "S")
+                wquant(n + AHEAD)
+                if quarters[n + AHEAD][2] == 1:
+                    spread(quarters[n + AHEAD][0], quarters[n + AHEAD][1])

@@ -157,6 +157,25 @@ def tile_vit_transformerblock_pa_kernel(
             nc.vector.bn_aggr(out=mean_var[:, t, :], in_=stats[:, t, :, :].rearrange("p s u -> p (s u)"))
             nc.scalar.activation(out=std[:, t : t + 1], in_=mean_var[:, t, 1:2], func=ACT.Sqrt, bias=eps[:, 0:1])
 
+        sums_s = const.tile([P, len(row_tiles)], F32)
+        negmean = const.tile([P, len(row_tiles)], F32)
+        ssq = const.tile([P, len(row_tiles)], F32)
+        junk = const.tile([P, FEATURES], BF16)
+
+        def stats_s1(t):
+            b, i = row_tiles[t]
+            nc.scalar.activation(out=junk[:], in_=x_rows[b][:, i, :], func=ACT.Identity, accum_out=sums_s[:, t : t + 1])
+            nc.scalar.activation(out=negmean[:, t : t + 1], in_=sums_s[:, t : t + 1], func=ACT.Copy, scale=-1.0 / FEATURES)
+
+        def stats_s2(t):
+            b, i = row_tiles[t]
+            nc.scalar.activation(out=junk[:], in_=x_rows[b][:, i, :], func=ACT.Square, bias=negmean[:, t : t + 1], accum_out=ssq[:, t : t + 1])
+            nc.scalar.activation(out=std[:, t : t + 1], in_=ssq[:, t : t + 1], func=ACT.Sqrt, scale=1.0 / FEATURES, bias=eps[:, 0:1])
+
+        def small_s(t):
+            nc.vector.reciprocal(out=rstd[:, t : t + 1], in_=std[:, t : t + 1])
+            nc.vector.tensor_tensor(out=shift[:, t : t + 1], in0=negmean[:, t : t + 1], in1=rstd[:, t : t + 1], op=ALU.mult)
+
         def small(t):
             nc.vector.reciprocal(out=rstd[:, t : t + 1], in_=std[:, t : t + 1])
             nc.vector.scalar_tensor_tensor(
@@ -211,7 +230,7 @@ def tile_vit_transformerblock_pa_kernel(
 
         def wreg(n, eng, lo=0, hi=BANK_COLS):
             m, g, c = quarters[n]
-            if lo == 0:
+            if n not in grouped_w:
                 grouped_w[n] = group_pool.tile([P, BANK_COLS, PACK], BF16, align_bytes=64, name="grouped")
             regroup(COPY[eng], grouped_w[n][:, lo:hi, :], w_rows[(m, c)][:, :, g * BANK_COLS + lo : g * BANK_COLS + hi])
 
@@ -219,6 +238,12 @@ def tile_vit_transformerblock_pa_kernel(
             m, g, c = quarters[n]
             cols = slice(g * BANK_COLS, (g + 1) * BANK_COLS)
             quantise(w_codes[m][:, c, cols], w_scales[m][:, c, cols], grouped_w[n])
+
+        gate_word = const.tile([P, 1], U32)
+
+        def gate(u):
+            m, g, c = quarters[u]
+            nc.gpsimd.tensor_copy(out=gate_word[:], in_=w_codes[m][:, c, g * BANK_COLS : g * BANK_COLS + 1])
 
         def spread(m, g):
             bias_cols = slice(m * OUT_COLS + g * BANK_COLS, m * OUT_COLS + (g + 1) * BANK_COLS)
@@ -241,11 +266,18 @@ def tile_vit_transformerblock_pa_kernel(
                 )
             sums_of[(n, i)] = sums
 
-        def add(n, i):
+        def add(n, i, eng="V"):
             m, g, b = products[n]
-            if i == 0:
+            if n not in results:
                 results[n] = out_pool.tile([P, GROUP_HEADS, ROW_TILES, HEAD_DIM], F32, name="result")
             bias_cols = bias_all[:, m * OUT_COLS + g * BANK_COLS : m * OUT_COLS + (g + 1) * BANK_COLS]
+            if eng == "SG":
+                nc.scalar.copy(out=results[n][:, :, i, :], in_=sums_of[(n, i)][:].rearrange("p (a d) -> p a d", a=GROUP_HEADS))
+                nc.gpsimd.tensor_tensor(
+                    out=results[n][:, :, i, :], in0=results[n][:, :, i, :],
+                    in1=bias_cols.rearrange("p (a d) -> p a d", a=GROUP_HEADS), op=ALU.add,
+                )
+                return
             nc.vector.tensor_tensor(
                 out=results[n][:, :, i, :], in0=sums_of[(n, i)][:].rearrange("p (a d) -> p a d", a=GROUP_HEADS),
                 in1=bias_cols.rearrange("p (a d) -> p a d", a=GROUP_HEADS), op=ALU.add,
@@ -258,10 +290,10 @@ def tile_vit_transformerblock_pa_kernel(
                 in_=results[n][:, :, lo:hi, :],
             )
 
-        def project(n, st=STORE_TILES):
+        def project(n, st=STORE_TILES, sg=()):
             for i in range(ROW_TILES):
                 mm(n, i)
-                add(n, i)
+                add(n, i, "SG" if i in sg else "V")
                 if (i + 1) % st == 0:
                     store(n, i + 1 - st, i + 1)
 
@@ -310,10 +342,33 @@ def tile_vit_transformerblock_pa_kernel(
         wreg(3, "S")
         wquant(3)
         spread(0, 1)
+
+        SS = 384
+        def unit_v(u):
+            if u < len(quarters) and SS < BANK_COLS:
+                wreg(u, "V", SS, BANK_COLS)
+        def unit_s(u):
+            if u < len(quarters):
+                wreg(u, "S", 0, SS)
+        def unit_done(u):
+            if u < len(quarters):
+                wquant(u)
+                if quarters[u][2] == 1:
+                    spread(quarters[u][0], quarters[u][1])
+        unit_v(1 + AHEAD)
         for n in range(1, len(products)):
-            project(n, ROW_TILES if n < len(products) - 1 else STORE_TILES)
-            if n + AHEAD < len(quarters):
-                wreg(n + AHEAD, "S")
-                wquant(n + AHEAD)
-                if quarters[n + AHEAD][2] == 1:
-                    spread(quarters[n + AHEAD][0], quarters[n + AHEAD][1])
+            for i in range(ROW_TILES):
+                mm(n, i)
+            if n - 1 + AHEAD < len(quarters):
+                gate(n - 1 + AHEAD)
+            add(n, 0, "SG")
+            unit_s(n + AHEAD)
+            for i in range(1, ROW_TILES):
+                add(n, i)
+            unit_v(n + AHEAD + 1)
+            unit_done(n + AHEAD)
+            if n < len(products) - 1:
+                store(n, 0, 4)
+            else:
+                store(n, 0, 2)
+                store(n, 2, 4)

@@ -31,6 +31,7 @@ RUN = 4
 AHEAD = 3
 STORE_TILES = 2
 
+X_ORDER = [(0, 0), (0, 1), (0, 2), (0, 3), (1, 3), (1, 0), (1, 1), (1, 2)]
 FLOPS = 2 * BATCHES * ROWS * FEATURES * 3 * OUT_COLS
 
 
@@ -60,13 +61,9 @@ def tile_vit_transformerblock_pa_kernel(
         sum_psum = ctx.enter_context(tc.psum_pool(name="sums", bufs=ROW_TILES))
         ctx.enter_context(tc.manual_schedule())
 
-        x_rows = []
-        for b in range(BATCHES):
-            x_sb = keep.tile([P, ROW_TILES, FEATURES], BF16, name="x_sb_%d" % b)
-            by_row_tile = x[b].rearrange("(p i) d -> i p d", i=ROW_TILES)
-            for i in range(ROW_TILES):
-                nc.sync.dma_start(out=x_sb[:, i, :], in_=by_row_tile[i])
-            x_rows.append(x_sb)
+        x_rows = [keep.tile([P, ROW_TILES, FEATURES], BF16, name="x_sb_%d" % b) for b in range(BATCHES)]
+        for b, i in X_ORDER:
+            nc.sync.dma_start(out=x_rows[b][:, i, :], in_=x[b].rearrange("(p i) d -> i p d", i=ROW_TILES)[i])
 
         w_rows = {}
         for m in range(3):
@@ -196,7 +193,10 @@ def tile_vit_transformerblock_pa_kernel(
             xhat_tiles[(b, i)] = xhat
 
         def flip(b, c, j):
-            flipped = flip_psum.tile([P, ROW_TILES, P], F32, tag="flip")
+            if (b, c) == (0, 1):
+                flipped = sum_psum.tile([P, ROW_TILES, P], F32, name="sums")
+            else:
+                flipped = flip_psum.tile([P, ROW_TILES, P], F32, tag="flip")
             for i in range(ROW_TILES):
                 nc.tensor.transpose(flipped[:, i, :], xhat_tiles[(b, i)][:, c, j, :], ident[:])
             flips[(b, c, j)] = flipped
@@ -220,7 +220,10 @@ def tile_vit_transformerblock_pa_kernel(
             grouped = group_pool.tile([P, BANK_COLS, PACK], BF16, align_bytes=64, name="grouped")
             w = BANK_COLS // pieces
             for k in range(pieces):
-                regroup(COPY[eng], grouped[:, k * w : (k + 1) * w, :], planes[(b, c)][:, :, k * w : (k + 1) * w])
+                if eng == "G":
+                    gp_copy(grouped[:, k * w : (k + 1) * w, :], planes[(b, c)][:, :, k * w : (k + 1) * w].rearrange("p j w -> p w j"))
+                else:
+                    regroup(COPY[eng], grouped[:, k * w : (k + 1) * w, :], planes[(b, c)][:, :, k * w : (k + 1) * w])
             grouped_h[(b, c)] = grouped
 
         def hquant(b, c):
@@ -297,23 +300,36 @@ def tile_vit_transformerblock_pa_kernel(
                 if (i + 1) % st == 0:
                     store(n, i + 1 - st, i + 1)
 
-        for t in range(8):
+        VT = [0,1,2,3,4,5,6]
+        SPLAN = {1: [(1, 7)], 2: [(2, 7)], 3: [(3, 7)], 4: [(4, 0)], 5: [(5, 0)], 6: [(6, 0)]}
+        def extra(k):
+            for what, ts in SPLAN.get(k, ()):
+                if what == 1:
+                    stats_s1(ts)
+                elif what == 2:
+                    stats_s2(ts)
+                elif what == 3:
+                    small_s(ts)
+                    xhat_of(ts, "S")
+                elif what == 4:
+                    wreg(0, "S", 0, 256)
+                elif what == 5:
+                    wreg(0, "S", 256, 512)
+                elif what == 6:
+                    for j in range(2):
+                        flip(0, 0, j)
+                        exit_h(0, 0, j, "S")
+        for k, t in enumerate(VT):
             bs(t, 0)
-            if t > 0:
-                small(t - 1)
-                xhat_of(t - 1, "G")
+            if k > 0:
+                small(VT[k - 1])
+                xhat_of(VT[k - 1], "G")
             bs(t, 1)
             aggr(t)
-            if t == 4:
-                wreg(0, "S", 0, 256)
-            if t == 5:
-                wreg(0, "S", 256, 512)
-            if t == 6:
-                for j in range(2):
-                    flip(0, 0, j)
-                    exit_h(0, 0, j, "S")
-        small(7)
-        xhat_of(7, "G")
+            extra(k)
+        small(VT[-1])
+        xhat_of(VT[-1], "G")
+        extra(99)
         for j in range(2, 4):
             flip(0, 0, j)
             exit_h(0, 0, j, "S")
@@ -332,8 +348,10 @@ def tile_vit_transformerblock_pa_kernel(
             for j in range(4):
                 flip(1, c, j)
                 exit_h(1, c, j, "S")
+            if c == 0:
+                gate(1)
+                hreg(1, 0, "G", 1)
         project(0, ROW_TILES)
-        hreg(1, 0, "V")
         hreg(1, 1, "V")
         wreg(2, "S")
         hquant(1, 0)

@@ -171,12 +171,15 @@ def tile_vit_transformerblock_pa_kernel(
 
         def small_s(t):
             nc.vector.reciprocal(out=rstd[:, t : t + 1], in_=std[:, t : t + 1])
-            nc.vector.tensor_tensor(out=shift[:, t : t + 1], in0=negmean[:, t : t + 1], in1=rstd[:, t : t + 1], op=ALU.mult)
+            nc.vector.tensor_scalar(
+                out=shift[:, t : t + 1], in0=negmean[:, t : t + 1], scalar1=rstd[:, t : t + 1], scalar2=1.0,
+                op0=ALU.mult, op1=ALU.mult,
+            )
 
         def small(t):
             nc.vector.reciprocal(out=rstd[:, t : t + 1], in_=std[:, t : t + 1])
-            nc.vector.scalar_tensor_tensor(
-                out=shift[:, t : t + 1], in0=mean_var[:, t, 0:1], scalar=-1.0, in1=rstd[:, t : t + 1],
+            nc.vector.tensor_scalar(
+                out=shift[:, t : t + 1], in0=mean_var[:, t, 0:1], scalar1=rstd[:, t : t + 1], scalar2=-1.0,
                 op0=ALU.mult, op1=ALU.mult,
             )
 

@@ -61,9 +61,30 @@ def tile_vit_transformerblock_pa_kernel(
         sum_psum = ctx.enter_context(tc.psum_pool(name="sums", bufs=ROW_TILES))
         ctx.enter_context(tc.manual_schedule())
 
+        eps = const.tile([P, 1], F32)
+        nc.vector.memset(eps[:], EPS)
+        warm = const.tile([P, 1], F32)
+        nc.scalar.activation(out=warm[:], in_=eps[:], func=ACT.Sqrt)
+        ident = const.tile([P, P], F32)
+        make_identity(nc, ident[:])
+        ident_bf = const.tile([P, P], BF16)
+        nc.scalar.copy(out=ident_bf[:], in_=ident[:])
+        bias_rows = const.tile([P, BANK_COLS], BF16)
+        nc.vector.memset(bias_rows[:].bitcast(I32), 0)
+
         x_rows = [keep.tile([P, ROW_TILES, FEATURES], BF16, name="x_sb_%d" % b) for b in range(BATCHES)]
         for b, i in X_ORDER:
             nc.sync.dma_start(out=x_rows[b][:, i, :], in_=x[b].rearrange("(p i) d -> i p d", i=ROW_TILES)[i])
+
+        gamma_bf = const.tile([P, PASSES, PACK], BF16)
+        beta_bf = const.tile([P, PASSES, PACK], BF16)
+        nc.sync.dma_start(out=gamma_bf[:], in_=gamma.rearrange("(c p j) -> p c j", c=PASSES, j=PACK))
+        nc.sync.dma_start(out=beta_bf[:], in_=beta.rearrange("(c p j) -> p c j", c=PASSES, j=PACK))
+        for m in range(3):
+            nc.sync.dma_start(
+                out=bias_rows[COL_GROUPS * m : COL_GROUPS * (m + 1), :],
+                in_=biases[m].rearrange("(g e) -> g e", g=COL_GROUPS),
+            )
 
         w_rows = {}
         for m in range(3):
@@ -77,34 +98,12 @@ def tile_vit_transformerblock_pa_kernel(
                 )
                 w_rows[(m, c)] = w_sb
 
-        gamma_bf = const.tile([P, PASSES, PACK], BF16)
-        beta_bf = const.tile([P, PASSES, PACK], BF16)
-        nc.scalar.dma_start(
-            out=gamma_bf[:], in_=gamma.rearrange("(c p j) -> p c j", c=PASSES, j=PACK)
-        )
-        nc.scalar.dma_start(
-            out=beta_bf[:], in_=beta.rearrange("(c p j) -> p c j", c=PASSES, j=PACK)
-        )
-        bias_rows = const.tile([P, 3 * OUT_COLS], BF16)
-        nc.gpsimd.memset(bias_rows[:], 0.0)
-        for m in range(3):
-            nc.scalar.dma_start(
-                out=bias_rows[0:1, m * OUT_COLS : (m + 1) * OUT_COLS],
-                in_=biases[m].rearrange("(o e) -> o e", o=1),
-            )
-
-        ident = const.tile([P, P], F32)
-        make_identity(nc, ident[:])
-        ones = const.tile([P, P], BF16)
-        nc.gpsimd.memset(ones[:], 1.0)
-        eps = const.tile([P, 1], F32)
-        nc.vector.memset(eps[:], EPS)
-        warm = const.tile([P, 1], F32)
-        nc.scalar.activation(out=warm[:], in_=eps[:], func=ACT.Sqrt)
         gamma_f = const.tile([P, PASSES * PACK], F32)
         beta_f = const.tile([P, PASSES * PACK], F32)
-        nc.scalar.copy(out=gamma_f[:], in_=gamma_bf[:].rearrange("p c j -> p (c j)"))
-        nc.scalar.copy(out=beta_f[:], in_=beta_bf[:].rearrange("p c j -> p (c j)"))
+
+        def cast_gamma_beta():
+            nc.scalar.copy(out=gamma_f[:], in_=gamma_bf[:].rearrange("p c j -> p (c j)"))
+            nc.scalar.copy(out=beta_f[:], in_=beta_bf[:].rearrange("p c j -> p (c j)"))
 
         h_codes = [
             keep.tile([P, PASSES, ROWS], U32, name="h_codes_%d" % b, align_bytes=64)
@@ -122,7 +121,7 @@ def tile_vit_transformerblock_pa_kernel(
             keep.tile([P, PASSES, OUT_COLS], U8, name="w_scales_%d" % m, align_bytes=64)
             for m in range(3)
         ]
-        bias_all = const.tile([P, 3 * OUT_COLS], F32)
+        bias_all = const.tile([P, 3 * OUT_COLS], BF16)
 
         def quantise(codes, scales, grouped):
             nc.vector.quantize_mx(
@@ -251,11 +250,15 @@ def tile_vit_transformerblock_pa_kernel(
             m, g, c = quarters[u]
             nc.gpsimd.tensor_copy(out=gate_word[:], in_=w_codes[m][:, c, g * BANK_COLS : g * BANK_COLS + 1])
 
-        def spread(m, g):
-            bias_cols = slice(m * OUT_COLS + g * BANK_COLS, m * OUT_COLS + (g + 1) * BANK_COLS)
-            sp = flip_psum.tile([P, BANK_COLS], F32, tag="flip")
-            nc.tensor.matmul(out=sp[:], lhsT=ones[:], rhs=bias_rows[:, bias_cols], start=True, stop=True)
-            nc.scalar.copy(out=bias_all[:, bias_cols], in_=sp[:])
+        def spread(m):
+            sp = flip_psum.tile([P, OUT_COLS], BF16, tag="flip")
+            for g in range(COL_GROUPS):
+                r = COL_GROUPS * m + g
+                nc.tensor.matmul(
+                    out=sp[:, g * BANK_COLS : (g + 1) * BANK_COLS], lhsT=ident_bf[:, r : r + 1].to_broadcast([P, P]),
+                    rhs=bias_rows[:], start=True, stop=True,
+                )
+            nc.scalar.copy(out=bias_all[:, m * OUT_COLS : (m + 1) * OUT_COLS], in_=sp[:])
 
         products = [(m, g, b) for m in range(3) for g in range(COL_GROUPS) for b in range(BATCHES)]
 
@@ -304,7 +307,7 @@ def tile_vit_transformerblock_pa_kernel(
                     store(n, i + 1 - st, i + 1)
 
         VT = [0,1,2,3,4,5,6]
-        SPLAN = {1: [(1, 7)], 2: [(2, 7)], 3: [(3, 7)], 4: [(4, 0)], 5: [(5, 0)], 6: [(6, 0)]}
+        SPLAN = {1: [(1, 7)], 2: [(2, 7)], 3: [(3, 7), (7, 0), (8, 0)], 4: [(4, 0)], 5: [(5, 0)], 6: [(6, 0)]}
         def extra(k):
             for what, ts in SPLAN.get(k, ()):
                 if what == 1:
@@ -314,6 +317,10 @@ def tile_vit_transformerblock_pa_kernel(
                 elif what == 3:
                     small_s(ts)
                     xhat_of(ts, "S")
+                elif what == 7:
+                    cast_gamma_beta()
+                elif what == 8:
+                    spread(0)
                 elif what == 4:
                     wreg(0, "S", 0, 256)
                 elif what == 5:
@@ -340,7 +347,6 @@ def tile_vit_transformerblock_pa_kernel(
             flip(0, 1, j)
             exit_h(0, 1, j, "V")
         wreg(1, "S")
-        spread(0, 0)
         hreg(0, 0, "V")
         hreg(0, 1, "V")
         wquant(0)
@@ -362,7 +368,6 @@ def tile_vit_transformerblock_pa_kernel(
         wquant(2)
         wreg(3, "S")
         wquant(3)
-        spread(0, 1)
 
         SS = 384
         def unit_v(u):
@@ -374,8 +379,8 @@ def tile_vit_transformerblock_pa_kernel(
         def unit_done(u):
             if u < len(quarters):
                 wquant(u)
-                if quarters[u][2] == 1:
-                    spread(quarters[u][0], quarters[u][1])
+                if quarters[u][1:] == (0, 1):
+                    spread(quarters[u][0])
         unit_v(1 + AHEAD)
         for n in range(1, len(products)):
             for i in range(ROW_TILES):

@@ -31,7 +31,7 @@ RUN = 4
 AHEAD = 3
 STORE_TILES = 2
 
-X_ORDER = [(0, 0), (0, 1), (0, 2), (0, 3), (1, 3), (1, 0), (1, 1), (1, 2)]
+X_ORDER = [(0, 0), (1, 3), (0, 1), (0, 2), (0, 3), (1, 0), (1, 1), (1, 2)]
 FLOPS = 2 * BATCHES * ROWS * FEATURES * 3 * OUT_COLS
 
 
@@ -55,7 +55,7 @@ def tile_vit_transformerblock_pa_kernel(
         keep = ctx.enter_context(tc.tile_pool(name="keep", bufs=1))
         xhat_pool = ctx.enter_context(tc.tile_pool(name="xhat", bufs=BATCHES * ROW_TILES))
         plane_pool = ctx.enter_context(tc.tile_pool(name="planes", bufs=4))
-        group_pool = ctx.enter_context(tc.tile_pool(name="grouped", bufs=4))
+        group_pool = ctx.enter_context(tc.tile_pool(name="grouped", bufs=6))
         out_pool = ctx.enter_context(tc.tile_pool(name="out", bufs=4))
         flip_psum = ctx.enter_context(tc.psum_pool(name="flip", bufs=4))
         sum_psum = ctx.enter_context(tc.psum_pool(name="sums", bufs=ROW_TILES))
@@ -73,18 +73,23 @@ def tile_vit_transformerblock_pa_kernel(
         nc.vector.memset(bias_rows[:].bitcast(I32), 0)
 
         x_rows = [keep.tile([P, ROW_TILES, FEATURES], BF16, name="x_sb_%d" % b) for b in range(BATCHES)]
-        for b, i in X_ORDER:
+        def load_x(b, i):
             nc.sync.dma_start(out=x_rows[b][:, i, :], in_=x[b].rearrange("(p i) d -> i p d", i=ROW_TILES)[i])
 
-        gamma_bf = const.tile([P, PASSES, PACK], BF16)
-        beta_bf = const.tile([P, PASSES, PACK], BF16)
-        nc.sync.dma_start(out=gamma_bf[:], in_=gamma.rearrange("(c p j) -> p c j", c=PASSES, j=PACK))
-        nc.sync.dma_start(out=beta_bf[:], in_=beta.rearrange("(c p j) -> p c j", c=PASSES, j=PACK))
+        for b, i in X_ORDER[:2]:
+            load_x(b, i)
         for m in range(3):
             nc.sync.dma_start(
                 out=bias_rows[COL_GROUPS * m : COL_GROUPS * (m + 1), :],
                 in_=biases[m].rearrange("(g e) -> g e", g=COL_GROUPS),
             )
+        for b, i in X_ORDER[2:]:
+            load_x(b, i)
+
+        gamma_bf = const.tile([P, PASSES, PACK], BF16)
+        beta_bf = const.tile([P, PASSES, PACK], BF16)
+        nc.sync.dma_start(out=gamma_bf[:], in_=gamma.rearrange("(c p j) -> p c j", c=PASSES, j=PACK))
+        nc.sync.dma_start(out=beta_bf[:], in_=beta.rearrange("(c p j) -> p c j", c=PASSES, j=PACK))
 
         w_rows = {}
         for m in range(3):
@@ -250,6 +255,8 @@ def tile_vit_transformerblock_pa_kernel(
             m, g, c = quarters[u]
             nc.gpsimd.tensor_copy(out=gate_word[:], in_=w_codes[m][:, c, g * BANK_COLS : g * BANK_COLS + 1])
 
+        spreads = {}
+
         def spread(m):
             sp = flip_psum.tile([P, OUT_COLS], BF16, tag="flip")
             for g in range(COL_GROUPS):
@@ -258,7 +265,10 @@ def tile_vit_transformerblock_pa_kernel(
                     out=sp[:, g * BANK_COLS : (g + 1) * BANK_COLS], lhsT=ident_bf[:, r : r + 1].to_broadcast([P, P]),
                     rhs=bias_rows[:], start=True, stop=True,
                 )
-            nc.scalar.copy(out=bias_all[:, m * OUT_COLS : (m + 1) * OUT_COLS], in_=sp[:])
+            spreads[m] = sp
+
+        def spread_copy(m):
+            nc.scalar.copy(out=bias_all[:, m * OUT_COLS : (m + 1) * OUT_COLS], in_=spreads[m][:])
 
         products = [(m, g, b) for m in range(3) for g in range(COL_GROUPS) for b in range(BATCHES)]
 
@@ -306,46 +316,82 @@ def tile_vit_transformerblock_pa_kernel(
                 if (i + 1) % st == 0:
                     store(n, i + 1 - st, i + 1)
 
-        VT = [0,1,2,3,4,5,6]
-        SPLAN = {1: [(1, 7)], 2: [(2, 7)], 3: [(3, 7), (7, 0), (8, 0)], 4: [(4, 0)], 5: [(5, 0)], 6: [(6, 0)]}
-        def extra(k):
-            for what, ts in SPLAN.get(k, ()):
-                if what == 1:
-                    stats_s1(ts)
-                elif what == 2:
-                    stats_s2(ts)
-                elif what == 3:
-                    small_s(ts)
-                    xhat_of(ts, "S")
-                elif what == 7:
-                    cast_gamma_beta()
-                elif what == 8:
-                    spread(0)
-                elif what == 4:
-                    wreg(0, "S", 0, 256)
-                elif what == 5:
-                    wreg(0, "S", 256, 512)
-                elif what == 6:
-                    for j in range(2):
-                        flip(0, 0, j)
-                        exit_h(0, 0, j, "S")
+
+        def aggr_v(t):
+            nc.vector.bn_aggr(out=mean_var[:, t, :], in_=stats[:, t, :, :].rearrange("p s u -> p (s u)"))
+            nc.scalar.activation(out=std[:, t : t + 1], in_=mean_var[:, t, 1:2], func=ACT.Sqrt, bias=eps[:, 0:1])
+
+        def recip(t):
+            nc.vector.reciprocal(out=rstd[:, t : t + 1], in_=std[:, t : t + 1])
+
+        def shift_v(t):
+            nc.vector.tensor_scalar(
+                out=shift[:, t : t + 1], in0=mean_var[:, t, 0:1], scalar1=rstd[:, t : t + 1], scalar2=-1.0,
+                op0=ALU.mult, op1=ALU.mult,
+            )
+
+        def shift_s(t):
+            nc.vector.tensor_scalar(
+                out=shift[:, t : t + 1], in0=negmean[:, t : t + 1], scalar1=rstd[:, t : t + 1], scalar2=1.0,
+                op0=ALU.mult, op1=ALU.mult,
+            )
+
+        def xhat_and_flip(t):
+            xhat_of(t, "G")
+            if t < ROW_TILES:
+                for c in range(PASSES):
+                    for j in range(PACK):
+                        nc.tensor.transpose(flips[(0, c, j)][:, t, :], xhat_tiles[(0, t)][:, c, j, :], ident[:])
+
+        spread(0)
+        for j in range(PACK):
+            flipped = flip_psum.tile([P, ROW_TILES, P], F32, tag="flip")
+            flips[(0, 0, j)] = flipped
+        for j in range(PACK):
+            flipped = sum_psum.tile([P, ROW_TILES, P], F32, name="sums")
+            flips[(0, 1, j)] = flipped
+        VT = [0, 1, 2, 3, 4, 5, 6]
+        ST = 7
+        SLOT = {"s1": 0, "s2": 1, "bias": 2, "xhat": 3, "cast": 3, "q0a": 4, "q0b": 5}
         for k, t in enumerate(VT):
             bs(t, 0)
-            if k > 0:
-                small(VT[k - 1])
-                xhat_of(VT[k - 1], "G")
+            if k >= 2:
+                shift_v(VT[k - 2])
+                xhat_and_flip(VT[k - 2])
+            if k >= 1:
+                aggr_v(VT[k - 1])
+            if k == SLOT["xhat"]:
+                recip(ST)
             bs(t, 1)
-            aggr(t)
-            extra(k)
-        small(VT[-1])
-        xhat_of(VT[-1], "G")
-        extra(99)
-        for j in range(2, 4):
-            flip(0, 0, j)
+            if k >= 1:
+                recip(VT[k - 1])
+            if k == SLOT["xhat"]:
+                shift_s(ST)
+                xhat_of(ST, "S")
+            if k == SLOT["s1"]:
+                stats_s1(ST)
+            if k == SLOT["s2"]:
+                stats_s2(ST)
+            if k == SLOT["bias"]:
+                spread_copy(0)
+            if k == SLOT["cast"]:
+                cast_gamma_beta()
+            if k == SLOT["q0a"]:
+                wreg(0, "S", 0, 256)
+            if k == SLOT["q0b"]:
+                wreg(0, "S", 256, 512)
+        shift_v(VT[-2])
+        xhat_and_flip(VT[-2])
+        aggr_v(VT[-1])
+        for j in range(4):
             exit_h(0, 0, j, "S")
         for j in range(4):
-            flip(0, 1, j)
             exit_h(0, 1, j, "V")
+            if j == 0:
+                recip(VT[-1])
+            if j == 1:
+                shift_v(VT[-1])
+                xhat_and_flip(VT[-1])
         wreg(1, "S")
         hreg(0, 0, "V")
         hreg(0, 1, "V")
@@ -353,6 +399,7 @@ def tile_vit_transformerblock_pa_kernel(
         hquant(0, 0)
         hquant(0, 1)
         wquant(1)
+        wreg(1 + AHEAD, "V", 384, BANK_COLS)
         for c in range(2):
             for j in range(4):
                 flip(1, c, j)
@@ -381,7 +428,7 @@ def tile_vit_transformerblock_pa_kernel(
                 wquant(u)
                 if quarters[u][1:] == (0, 1):
                     spread(quarters[u][0])
-        unit_v(1 + AHEAD)
+                    spread_copy(quarters[u][0])
         for n in range(1, len(products)):
             for i in range(ROW_TILES):
                 mm(n, i)

@@ -192,7 +192,7 @@ def tile_vit_transformerblock_pa_kernel(
             xhat = xhat_pool.tile([P, PASSES, PACK, P], F32, name="xhat")
             src = x_rows[b][:, i, :].rearrange("p (c q j) -> p c j q", c=PASSES, j=PACK)
             if eng == "G":
-                nc.gpsimd.tensor_scalar(out=xhat[:], in0=src, scalar1=rstd[:, t : t + 1], scalar2=shift[:, t : t + 1], op0=ALU.mult, op1=ALU.add)
+                nc.gpsimd.tensor_scalar(out=xhat[:], in0=src, scalar1=negmean[:, t : t + 1], scalar2=rstd[:, t : t + 1], op0=ALU.add, op1=ALU.mult)
             elif eng == "V":
                 nc.vector.tensor_scalar(out=xhat[:], in0=src, scalar1=rstd[:, t : t + 1], scalar2=shift[:, t : t + 1], op0=ALU.mult, op1=ALU.add)
             else:
@@ -320,6 +320,7 @@ def tile_vit_transformerblock_pa_kernel(
         def aggr_v(t):
             nc.vector.bn_aggr(out=mean_var[:, t, :], in_=stats[:, t, :, :].rearrange("p s u -> p (s u)"))
             nc.scalar.activation(out=std[:, t : t + 1], in_=mean_var[:, t, 1:2], func=ACT.Sqrt, bias=eps[:, 0:1])
+            nc.scalar.activation(out=negmean[:, t : t + 1], in_=mean_var[:, t, 0:1], func=ACT.Copy, scale=-1.0)
 
         def recip(t):
             nc.vector.reciprocal(out=rstd[:, t : t + 1], in_=std[:, t : t + 1])
@@ -331,10 +332,7 @@ def tile_vit_transformerblock_pa_kernel(
             )
 
         def shift_s(t):
-            nc.vector.tensor_scalar(
-                out=shift[:, t : t + 1], in0=negmean[:, t : t + 1], scalar1=rstd[:, t : t + 1], scalar2=1.0,
-                op0=ALU.mult, op1=ALU.mult,
-            )
+            nc.scalar.activation(out=shift[:, t : t + 1], in_=negmean[:, t : t + 1], func=ACT.Identity, scale=rstd[:, t : t + 1])
 
         def xhat_and_flip(t):
             xhat_of(t, "G")
@@ -355,9 +353,6 @@ def tile_vit_transformerblock_pa_kernel(
         SLOT = {"s1": 0, "s2": 1, "bias": 2, "xhat": 3, "cast": 3, "q0a": 4, "q0b": 5}
         for k, t in enumerate(VT):
             bs(t, 0)
-            if k >= 2:
-                shift_v(VT[k - 2])
-                xhat_and_flip(VT[k - 2])
             if k >= 1:
                 aggr_v(VT[k - 1])
             if k == SLOT["xhat"]:
@@ -365,6 +360,7 @@ def tile_vit_transformerblock_pa_kernel(
             bs(t, 1)
             if k >= 1:
                 recip(VT[k - 1])
+                xhat_and_flip(VT[k - 1])
             if k == SLOT["xhat"]:
                 shift_s(ST)
                 xhat_of(ST, "S")
@@ -380,8 +376,6 @@ def tile_vit_transformerblock_pa_kernel(
                 wreg(0, "S", 0, 256)
             if k == SLOT["q0b"]:
                 wreg(0, "S", 256, 512)
-        shift_v(VT[-2])
-        xhat_and_flip(VT[-2])
         aggr_v(VT[-1])
         for j in range(4):
             exit_h(0, 0, j, "S")
@@ -389,8 +383,6 @@ def tile_vit_transformerblock_pa_kernel(
             exit_h(0, 1, j, "V")
             if j == 0:
                 recip(VT[-1])
-            if j == 1:
-                shift_v(VT[-1])
                 xhat_and_flip(VT[-1])
         wreg(1, "S")
         hreg(0, 0, "V")

@@ -29,6 +29,7 @@ STATS_CHUNK = 512
 STATS_CHUNKS = FEATURES // STATS_CHUNK
 RUN = 4
 AHEAD = 3
+TAIL_COLS = 256
 STORE_TILES = 2
 
 X_ORDER = [(0, 0), (1, 3), (0, 1), (0, 2), (0, 3), (1, 0), (1, 1), (1, 2)]
@@ -53,10 +54,11 @@ def tile_vit_transformerblock_pa_kernel(
     with ExitStack() as ctx:
         const = ctx.enter_context(tc.tile_pool(name="const", bufs=1))
         keep = ctx.enter_context(tc.tile_pool(name="keep", bufs=1))
-        xhat_pool = ctx.enter_context(tc.tile_pool(name="xhat", bufs=BATCHES * ROW_TILES))
+        xhat_pool = ctx.enter_context(tc.tile_pool(name="xhat", bufs=6))
         plane_pool = ctx.enter_context(tc.tile_pool(name="planes", bufs=4))
-        group_pool = ctx.enter_context(tc.tile_pool(name="grouped", bufs=6))
-        out_pool = ctx.enter_context(tc.tile_pool(name="out", bufs=4))
+        group_pool = ctx.enter_context(tc.tile_pool(name="grouped", bufs=4))
+        wgroup_pool = ctx.enter_context(tc.tile_pool(name="wgrouped", bufs=3))
+        out_pool = ctx.enter_context(tc.tile_pool(name="out", bufs=5))
         flip_psum = ctx.enter_context(tc.psum_pool(name="flip", bufs=4))
         sum_psum = ctx.enter_context(tc.psum_pool(name="sums", bufs=ROW_TILES))
         ctx.enter_context(tc.manual_schedule())
@@ -78,11 +80,7 @@ def tile_vit_transformerblock_pa_kernel(
 
         for b, i in X_ORDER[:2]:
             load_x(b, i)
-        for m in range(3):
-            nc.sync.dma_start(
-                out=bias_rows[COL_GROUPS * m : COL_GROUPS * (m + 1), :],
-                in_=biases[m].rearrange("(g e) -> g e", g=COL_GROUPS),
-            )
+        nc.sync.dma_start(out=bias_rows[0:COL_GROUPS, :], in_=biases[0].rearrange("(g e) -> g e", g=COL_GROUPS))
         for b, i in X_ORDER[2:]:
             load_x(b, i)
 
@@ -103,6 +101,10 @@ def tile_vit_transformerblock_pa_kernel(
                 )
                 w_rows[(m, c)] = w_sb
 
+        bias_all = [const.tile([P, OUT_COLS], BF16, name="bias_all_%d" % m) for m in range(3)]
+        for m in range(1, 3):
+            nc.sync.dma_start(out=bias_all[m][:], in_=biases[m].partition_broadcast(P))
+
         gamma_f = const.tile([P, PASSES * PACK], F32)
         beta_f = const.tile([P, PASSES * PACK], F32)
 
@@ -118,21 +120,23 @@ def tile_vit_transformerblock_pa_kernel(
             keep.tile([P, PASSES, ROWS], U8, name="h_scales_%d" % b, align_bytes=64)
             for b in range(BATCHES)
         ]
+        units = [(m, g * BANK_COLS, BANK_COLS) for m in range(3) for g in range(COL_GROUPS)]
+        m, col, width = units.pop()
+        units += [(m, col + i * TAIL_COLS, TAIL_COLS) for i in range(width // TAIL_COLS)]
         w_codes = [
-            keep.tile([P, PASSES, OUT_COLS], U32, name="w_codes_%d" % m, align_bytes=64)
-            for m in range(3)
+            keep.tile([P, PASSES, width], U32, name="w_codes_%d" % k, align_bytes=64)
+            for k, (m, col, width) in enumerate(units)
         ]
         w_scales = [
-            keep.tile([P, PASSES, OUT_COLS], U8, name="w_scales_%d" % m, align_bytes=64)
-            for m in range(3)
+            keep.tile([P, PASSES, width], U8, name="w_scales_%d" % k, align_bytes=64)
+            for k, (m, col, width) in enumerate(units)
         ]
-        bias_all = const.tile([P, 3 * OUT_COLS], BF16)
 
         def quantise(codes, scales, grouped):
             nc.vector.quantize_mx(
                 out=codes.bitcast(FP8X4),
                 scales=scales,
-                in_=grouped[:].rearrange("p w j -> p (w j)"),
+                in_=grouped.rearrange("p w j -> p (w j)"),
             )
 
 
@@ -234,26 +238,38 @@ def tile_vit_transformerblock_pa_kernel(
             grouped_h[(b, c)] = grouped
 
         def hquant(b, c):
-            quantise(h_codes[b][:, c, :], h_scales[b][:, c, :], grouped_h[(b, c)])
+            quantise(h_codes[b][:, c, :], h_scales[b][:, c, :], grouped_h[(b, c)][:])
 
-        quarters = [(m, g, c) for m in range(3) for g in range(COL_GROUPS) for c in range(PASSES)]
+        quarters = [(k, c) for k in range(len(units)) for c in range(PASSES)]
 
         def wreg(n, eng, lo=0, hi=BANK_COLS):
-            m, g, c = quarters[n]
-            if n not in grouped_w:
-                grouped_w[n] = group_pool.tile([P, BANK_COLS, PACK], BF16, align_bytes=64, name="grouped")
-            regroup(COPY[eng], grouped_w[n][:, lo:hi, :], w_rows[(m, c)][:, :, g * BANK_COLS + lo : g * BANK_COLS + hi])
+            k, c = quarters[n]
+            m, col, width = units[k]
+            lo, hi = lo * width // BANK_COLS, hi * width // BANK_COLS
+            if k not in grouped_w:
+                grouped_w[k] = wgroup_pool.tile([P, PASSES, width, PACK], BF16, align_bytes=64, name="wgrouped")
+            rows = w_rows[(m, c)][:, :, col + lo : col + hi]
+            if eng == "G":
+                gp_copy(grouped_w[k][:, c, lo:hi, :], rows.rearrange("p j w -> p w j"))
+            else:
+                regroup(COPY[eng], grouped_w[k][:, c, lo:hi, :], rows)
 
         def wquant(n):
-            m, g, c = quarters[n]
-            cols = slice(g * BANK_COLS, (g + 1) * BANK_COLS)
-            quantise(w_codes[m][:, c, cols], w_scales[m][:, c, cols], grouped_w[n])
+            k, c = quarters[n]
+            quantise(w_codes[k][:, c, :], w_scales[k][:, c, :], grouped_w[k][:, c, :, :])
+
+        def uquant(k):
+            nc.vector.quantize_mx(
+                out=w_codes[k][:].rearrange("p c w -> p (c w)").bitcast(FP8X4),
+                scales=w_scales[k][:].rearrange("p c w -> p (c w)"),
+                in_=grouped_w[k][:].rearrange("p c w j -> p (c w j)"),
+            )
 
         gate_word = const.tile([P, 1], U32)
 
         def gate(u):
-            m, g, c = quarters[u]
-            nc.gpsimd.tensor_copy(out=gate_word[:], in_=w_codes[m][:, c, g * BANK_COLS : g * BANK_COLS + 1])
+            k, c = quarters[u]
+            nc.gpsimd.tensor_copy(out=gate_word[:], in_=w_codes[k][:, c, 0:1])
 
         spreads = {}
 
@@ -268,54 +284,49 @@ def tile_vit_transformerblock_pa_kernel(
             spreads[m] = sp
 
         def spread_copy(m):
-            nc.scalar.copy(out=bias_all[:, m * OUT_COLS : (m + 1) * OUT_COLS], in_=spreads[m][:])
+            nc.scalar.copy(out=bias_all[m][:], in_=spreads[m][:])
 
-        products = [(m, g, b) for m in range(3) for g in range(COL_GROUPS) for b in range(BATCHES)]
+        products = [(k, b) for k in range(len(units)) for b in range(BATCHES)]
 
-        def mm(n, i):
-            m, g, b = products[n]
-            cols = slice(g * BANK_COLS, (g + 1) * BANK_COLS)
+        def mm(n, i, c):
+            k, b = products[n]
+            m, col, width = units[k]
             rows = slice(i * P, (i + 1) * P)
-            sums = sum_psum.tile([P, BANK_COLS], F32, name="sums")
-            for c in range(PASSES):
-                nc.tensor.matmul_mx(
-                    out=sums[:], lhsT=h_codes[b][:, c, rows].bitcast(FP8X4), lhsT_scale=h_scales[b][:, c, rows],
-                    rhs=w_codes[m][:, c, cols].bitcast(FP8X4), rhs_scale=w_scales[m][:, c, cols],
-                    start=(c == 0), stop=(c == PASSES - 1),
-                )
-            sums_of[(n, i)] = sums
+            if c == 0:
+                if n > 0 and i == 0:
+                    sums = flip_psum.tile([P, width], F32, tag="flip")
+                else:
+                    sums = sum_psum.tile([P, width], F32, name="sums")
+                sums_of[(n, i)] = sums
+            nc.tensor.matmul_mx(
+                out=sums_of[(n, i)][:], lhsT=h_codes[b][:, c, rows].bitcast(FP8X4), lhsT_scale=h_scales[b][:, c, rows],
+                rhs=w_codes[k][:, c, :].bitcast(FP8X4), rhs_scale=w_scales[k][:, c, :],
+                start=(c == 0), stop=(c == PASSES - 1),
+            )
 
         def add(n, i, eng="V"):
-            m, g, b = products[n]
+            k, b = products[n]
+            m, col, width = units[k]
+            heads = width // HEAD_DIM
             if n not in results:
-                results[n] = out_pool.tile([P, GROUP_HEADS, ROW_TILES, HEAD_DIM], F32, name="result")
-            bias_cols = bias_all[:, m * OUT_COLS + g * BANK_COLS : m * OUT_COLS + (g + 1) * BANK_COLS]
+                results[n] = out_pool.tile([P, heads, ROW_TILES, HEAD_DIM], F32, name="result")
+            bias_cols = bias_all[m][:, col : col + width].rearrange("p (a d) -> p a d", a=heads)
+            sums = sums_of[(n, i)][:].rearrange("p (a d) -> p a d", a=heads)
+            result = results[n][:, :, i, :]
             if eng == "SG":
-                nc.scalar.copy(out=results[n][:, :, i, :], in_=sums_of[(n, i)][:].rearrange("p (a d) -> p a d", a=GROUP_HEADS))
-                nc.gpsimd.tensor_tensor(
-                    out=results[n][:, :, i, :], in0=results[n][:, :, i, :],
-                    in1=bias_cols.rearrange("p (a d) -> p a d", a=GROUP_HEADS), op=ALU.add,
-                )
-                return
-            nc.vector.tensor_tensor(
-                out=results[n][:, :, i, :], in0=sums_of[(n, i)][:].rearrange("p (a d) -> p a d", a=GROUP_HEADS),
-                in1=bias_cols.rearrange("p (a d) -> p a d", a=GROUP_HEADS), op=ALU.add,
-            )
+                nc.scalar.copy(out=result, in_=sums)
+                nc.gpsimd.tensor_tensor(out=result, in0=result, in1=bias_cols, op=ALU.add)
+            else:
+                nc.vector.tensor_tensor(out=result, in0=sums, in1=bias_cols, op=ALU.add)
 
         def store(n, lo, hi):
-            m, g, b = products[n]
+            k, b = products[n]
+            m, col, width = units[k]
+            first = col // HEAD_DIM
             nc.sync.dma_start(
-                out=outs[m][b, g * GROUP_HEADS : (g + 1) * GROUP_HEADS].rearrange("a (p i) d -> p a i d", i=ROW_TILES)[:, :, lo:hi, :],
+                out=outs[m][b, first : first + width // HEAD_DIM].rearrange("a (p i) d -> p a i d", i=ROW_TILES)[:, :, lo:hi, :],
                 in_=results[n][:, :, lo:hi, :],
             )
-
-        def project(n, st=STORE_TILES, sg=()):
-            for i in range(ROW_TILES):
-                mm(n, i)
-                add(n, i, "SG" if i in sg else "V")
-                if (i + 1) % st == 0:
-                    store(n, i + 1 - st, i + 1)
-
 
         def aggr_v(t):
             nc.vector.bn_aggr(out=mean_var[:, t, :], in_=stats[:, t, :, :].rearrange("p s u -> p (s u)"))
@@ -341,6 +352,12 @@ def tile_vit_transformerblock_pa_kernel(
                     for j in range(PACK):
                         nc.tensor.transpose(flips[(0, c, j)][:, t, :], xhat_tiles[(0, t)][:, c, j, :], ident[:])
 
+        def sflip():
+            if ST < ROW_TILES:
+                for c in range(PASSES):
+                    for j in range(PACK):
+                        nc.tensor.transpose(flips[(0, c, j)][:, ST, :], xhat_tiles[(0, ST)][:, c, j, :], ident[:])
+
         spread(0)
         for j in range(PACK):
             flipped = flip_psum.tile([P, ROW_TILES, P], F32, tag="flip")
@@ -348,7 +365,7 @@ def tile_vit_transformerblock_pa_kernel(
         for j in range(PACK):
             flipped = sum_psum.tile([P, ROW_TILES, P], F32, name="sums")
             flips[(0, 1, j)] = flipped
-        VT = [0, 1, 2, 3, 4, 5, 6]
+        VT = [t for t in range(8) if t != 7]
         ST = 7
         SLOT = {"s1": 0, "s2": 1, "bias": 2, "xhat": 3, "cast": 3, "q0a": 4, "q0b": 5}
         for k, t in enumerate(VT):
@@ -364,6 +381,7 @@ def tile_vit_transformerblock_pa_kernel(
             if k == SLOT["xhat"]:
                 shift_s(ST)
                 xhat_of(ST, "S")
+                sflip()
             if k == SLOT["s1"]:
                 stats_s1(ST)
             if k == SLOT["s2"]:
@@ -386,54 +404,51 @@ def tile_vit_transformerblock_pa_kernel(
                 xhat_and_flip(VT[-1])
         wreg(1, "S")
         hreg(0, 0, "V")
-        hreg(0, 1, "V")
         wquant(0)
         hquant(0, 0)
-        hquant(0, 1)
+        hreg(0, 1, "V")
         wquant(1)
-        wreg(1 + AHEAD, "V", 384, BANK_COLS)
+        hquant(0, 1)
+        for j in range(4):
+            flip(1, 0, j)
+            exit_h(1, 0, j, "S")
+        gate(1)
+        hreg(1, 0, "G", 1)
         for c in range(2):
-            for j in range(4):
-                flip(1, c, j)
-                exit_h(1, c, j, "S")
-            if c == 0:
-                gate(1)
-                hreg(1, 0, "G", 1)
-        project(0, ROW_TILES)
-        hreg(1, 1, "V")
+            for i in range(4):
+                mm(0, i, c)
         wreg(2, "S")
+        for j in range(4):
+            flip(1, 1, j)
+            exit_h(1, 1, j, "S")
+        for i in range(4):
+            add(0, i)
+        store(0, 0, 4)
         hquant(1, 0)
-        hquant(1, 1)
-        wquant(2)
+        for i in range(4):
+            mm(1, i, 0)
+        hreg(1, 1, "V")
         wreg(3, "S")
-        wquant(3)
+        hquant(1, 1)
+        for i in range(4):
+            mm(1, i, 1)
+        uquant(1)
 
-        SS = 384
-        def unit_v(u):
-            if u < len(quarters) and SS < BANK_COLS:
-                wreg(u, "V", SS, BANK_COLS)
-        def unit_s(u):
-            if u < len(quarters):
-                wreg(u, "S", 0, SS)
-        def unit_done(u):
-            if u < len(quarters):
-                wquant(u)
-                if quarters[u][1:] == (0, 1):
-                    spread(quarters[u][0])
-                    spread_copy(quarters[u][0])
+        S_END = 384
         for n in range(1, len(products)):
-            for i in range(ROW_TILES):
-                mm(n, i)
-            if n - 1 + AHEAD < len(quarters):
-                gate(n - 1 + AHEAD)
+            u = n + AHEAD
+            if n > 1:
+                for i in range(ROW_TILES):
+                    for c in range(PASSES):
+                        mm(n, i, c)
+            if u < len(quarters):
+
+                wreg(u, "G", S_END, BANK_COLS)
             add(n, 0, "SG")
-            unit_s(n + AHEAD)
+            if u < len(quarters):
+                wreg(u, "S", 0, S_END)
             for i in range(1, ROW_TILES):
                 add(n, i)
-            unit_v(n + AHEAD + 1)
-            unit_done(n + AHEAD)
-            if n < len(products) - 1:
-                store(n, 0, 4)
-            else:
-                store(n, 0, 2)
-                store(n, 2, 4)
+            if u < len(quarters) and quarters[u][1] == PASSES - 1:
+                uquant(quarters[u][0])
+            store(n, 0, ROW_TILES)

@@ -28,6 +28,7 @@ GROUP_HEADS = BANK_COLS // HEAD_DIM
 STATS_CHUNK = 512
 STATS_CHUNKS = FEATURES // STATS_CHUNK
 RUN = 4
+Q4_EARLY = 128
 AHEAD = 3
 TAIL_COLS = 256
 STORE_TILES = 2
@@ -69,10 +70,6 @@ def tile_vit_transformerblock_pa_kernel(
         nc.scalar.activation(out=warm[:], in_=eps[:], func=ACT.Sqrt)
         ident = const.tile([P, P], F32)
         make_identity(nc, ident[:])
-        ident_bf = const.tile([P, P], BF16)
-        nc.scalar.copy(out=ident_bf[:], in_=ident[:])
-        bias_rows = const.tile([P, BANK_COLS], BF16)
-        nc.vector.memset(bias_rows[:].bitcast(I32), 0)
 
         x_rows = [keep.tile([P, ROW_TILES, FEATURES], BF16, name="x_sb_%d" % b) for b in range(BATCHES)]
         def load_x(b, i):
@@ -80,7 +77,6 @@ def tile_vit_transformerblock_pa_kernel(
 
         for b, i in X_ORDER[:2]:
             load_x(b, i)
-        nc.sync.dma_start(out=bias_rows[0:COL_GROUPS, :], in_=biases[0].rearrange("(g e) -> g e", g=COL_GROUPS))
         for b, i in X_ORDER[2:]:
             load_x(b, i)
 
@@ -90,7 +86,10 @@ def tile_vit_transformerblock_pa_kernel(
         nc.sync.dma_start(out=beta_bf[:], in_=beta.rearrange("(c p j) -> p c j", c=PASSES, j=PACK))
 
         w_rows = {}
+        bias_all = [const.tile([P, OUT_COLS], BF16, name="bias_all_%d" % m) for m in range(3)]
         for m in range(3):
+            if m == 1:
+                nc.sync.dma_start(out=bias_all[0][:], in_=biases[0].partition_broadcast(P))
             for c in range(PASSES):
                 w_sb = keep.tile([P, PACK, OUT_COLS], BF16, name="w_sb_%d_%d" % (m, c))
                 nc.sync.dma_start(
@@ -101,7 +100,6 @@ def tile_vit_transformerblock_pa_kernel(
                 )
                 w_rows[(m, c)] = w_sb
 
-        bias_all = [const.tile([P, OUT_COLS], BF16, name="bias_all_%d" % m) for m in range(3)]
         for m in range(1, 3):
             nc.sync.dma_start(out=bias_all[m][:], in_=biases[m].partition_broadcast(P))
 
@@ -258,33 +256,11 @@ def tile_vit_transformerblock_pa_kernel(
             k, c = quarters[n]
             quantise(w_codes[k][:, c, :], w_scales[k][:, c, :], grouped_w[k][:, c, :, :])
 
-        def uquant(k):
-            nc.vector.quantize_mx(
-                out=w_codes[k][:].rearrange("p c w -> p (c w)").bitcast(FP8X4),
-                scales=w_scales[k][:].rearrange("p c w -> p (c w)"),
-                in_=grouped_w[k][:].rearrange("p c w j -> p (c w j)"),
-            )
-
         gate_word = const.tile([P, 1], U32)
 
         def gate(u):
             k, c = quarters[u]
             nc.gpsimd.tensor_copy(out=gate_word[:], in_=w_codes[k][:, c, 0:1])
-
-        spreads = {}
-
-        def spread(m):
-            sp = flip_psum.tile([P, OUT_COLS], BF16, tag="flip")
-            for g in range(COL_GROUPS):
-                r = COL_GROUPS * m + g
-                nc.tensor.matmul(
-                    out=sp[:, g * BANK_COLS : (g + 1) * BANK_COLS], lhsT=ident_bf[:, r : r + 1].to_broadcast([P, P]),
-                    rhs=bias_rows[:], start=True, stop=True,
-                )
-            spreads[m] = sp
-
-        def spread_copy(m):
-            nc.scalar.copy(out=bias_all[m][:], in_=spreads[m][:])
 
         products = [(k, b) for k in range(len(units)) for b in range(BATCHES)]
 
@@ -358,7 +334,6 @@ def tile_vit_transformerblock_pa_kernel(
                     for j in range(PACK):
                         nc.tensor.transpose(flips[(0, c, j)][:, ST, :], xhat_tiles[(0, ST)][:, c, j, :], ident[:])
 
-        spread(0)
         for j in range(PACK):
             flipped = flip_psum.tile([P, ROW_TILES, P], F32, tag="flip")
             flips[(0, 0, j)] = flipped
@@ -386,8 +361,6 @@ def tile_vit_transformerblock_pa_kernel(
                 stats_s1(ST)
             if k == SLOT["s2"]:
                 stats_s2(ST)
-            if k == SLOT["bias"]:
-                spread_copy(0)
             if k == SLOT["cast"]:
                 cast_gamma_beta()
             if k == SLOT["q0a"]:
@@ -427,14 +400,16 @@ def tile_vit_transformerblock_pa_kernel(
         hquant(1, 0)
         for i in range(4):
             mm(1, i, 0)
+        wquant(2)
         hreg(1, 1, "V")
         wreg(3, "S")
+        wreg(4, "S", 0, Q4_EARLY)
         hquant(1, 1)
         for i in range(4):
             mm(1, i, 1)
-        uquant(1)
+        wquant(3)
 
-        S_END = 384
+        S_END = 368
         for n in range(1, len(products)):
             u = n + AHEAD
             if n > 1:
@@ -442,13 +417,12 @@ def tile_vit_transformerblock_pa_kernel(
                     for c in range(PASSES):
                         mm(n, i, c)
             if u < len(quarters):
-
                 wreg(u, "G", S_END, BANK_COLS)
             add(n, 0, "SG")
             if u < len(quarters):
-                wreg(u, "S", 0, S_END)
+                wreg(u, "S", Q4_EARLY if n == 1 else 0, S_END)
             for i in range(1, ROW_TILES):
                 add(n, i)
-            if u < len(quarters) and quarters[u][1] == PASSES - 1:
-                uquant(quarters[u][0])
+            if u < len(quarters):
+                wquant(u)
             store(n, 0, ROW_TILES)

@@ -409,7 +409,7 @@ def tile_vit_transformerblock_pa_kernel(
             mm(1, i, 1)
         wquant(3)
 
-        S_END = 368
+        S_END = 448
         for n in range(1, len(products)):
             u = n + AHEAD
             if n > 1:

@@ -409,7 +409,7 @@ def tile_vit_transformerblock_pa_kernel(
             mm(1, i, 1)
         wquant(3)
 
-        S_END = 448
+        S_END = 416
         for n in range(1, len(products)):
             u = n + AHEAD
             if n > 1:

from contextlib import ExitStack

import concourse.mybir as mybir
from concourse.masks import make_identity

F32 = mybir.dt.float32
BF16 = mybir.dt.bfloat16
U32 = mybir.dt.uint32
U8 = mybir.dt.uint8
I32 = mybir.dt.int32
FP8X4 = mybir.dt.float8_e4m3fn_x4
ACT = mybir.ActivationFunctionType
ALU = mybir.AluOpType

P = 128
PACK = 4
K_PASS = P * PACK

BATCHES, ROWS, FEATURES, HEAD_DIM = 2, 512, 1024, 128
OUT_COLS = 1024
EPS = 1e-5

PASSES = FEATURES // K_PASS
ROW_TILES = ROWS // P
BANK_COLS = 512
COL_GROUPS = OUT_COLS // BANK_COLS
GROUP_HEADS = BANK_COLS // HEAD_DIM
STATS_CHUNK = 512
STATS_CHUNKS = FEATURES // STATS_CHUNK
RUN = 4
Q4_EARLY = 128
AHEAD = 3
TAIL_COLS = 256
STORE_TILES = 2

X_ORDER = [(0, 0), (1, 3), (0, 1), (0, 2), (0, 3), (1, 0), (1, 1), (1, 2)]
FLOPS = 2 * BATCHES * ROWS * FEATURES * 3 * OUT_COLS


def regroup(copy, grouped, rows):
    copy(
        out=grouped.rearrange("p (w r) j -> p w j r", r=RUN),
        in_=rows.rearrange("p j (w r) -> p w j r", r=RUN),
    )


def tile_vit_transformerblock_pa_kernel(
    tc, x, gamma, beta, Wq, bq, Wk, bk, Wv, bv, out_0, out_1, out_2
):
    nc = tc.nc
    weights = (Wq, Wk, Wv)
    biases = (bq, bk, bv)
    outs = (out_0, out_1, out_2)

    with ExitStack() as ctx:
        const = ctx.enter_context(tc.tile_pool(name="const", bufs=1))
        keep = ctx.enter_context(tc.tile_pool(name="keep", bufs=1))
        xhat_pool = ctx.enter_context(tc.tile_pool(name="xhat", bufs=6))
        plane_pool = ctx.enter_context(tc.tile_pool(name="planes", bufs=4))
        group_pool = ctx.enter_context(tc.tile_pool(name="grouped", bufs=4))
        wgroup_pool = ctx.enter_context(tc.tile_pool(name="wgrouped", bufs=3))
        out_pool = ctx.enter_context(tc.tile_pool(name="out", bufs=5))
        flip_psum = ctx.enter_context(tc.psum_pool(name="flip", bufs=4))
        sum_psum = ctx.enter_context(tc.psum_pool(name="sums", bufs=ROW_TILES))
        ctx.enter_context(tc.manual_schedule())

        eps = const.tile([P, 1], F32)
        nc.vector.memset(eps[:], EPS)
        warm = const.tile([P, 1], F32)
        nc.scalar.activation(out=warm[:], in_=eps[:], func=ACT.Sqrt)
        ident = const.tile([P, P], F32)
        make_identity(nc, ident[:])

        x_rows = [keep.tile([P, ROW_TILES, FEATURES], BF16, name="x_sb_%d" % b) for b in range(BATCHES)]
        def load_x(b, i):
            nc.sync.dma_start(out=x_rows[b][:, i, :], in_=x[b].rearrange("(p i) d -> i p d", i=ROW_TILES)[i])

        for b, i in X_ORDER[:2]:
            load_x(b, i)
        for b, i in X_ORDER[2:]:
            load_x(b, i)

        gamma_bf = const.tile([P, PASSES, PACK], BF16)
        beta_bf = const.tile([P, PASSES, PACK], BF16)
        nc.sync.dma_start(out=gamma_bf[:], in_=gamma.rearrange("(c p j) -> p c j", c=PASSES, j=PACK))
        nc.sync.dma_start(out=beta_bf[:], in_=beta.rearrange("(c p j) -> p c j", c=PASSES, j=PACK))

        w_rows = {}
        bias_all = [const.tile([P, OUT_COLS], BF16, name="bias_all_%d" % m) for m in range(3)]
        for m in range(3):
            if m == 1:
                nc.sync.dma_start(out=bias_all[0][:], in_=biases[0].partition_broadcast(P))
            for c in range(PASSES):
                w_sb = keep.tile([P, PACK, OUT_COLS], BF16, name="w_sb_%d_%d" % (m, c))
                nc.sync.dma_start(
                    out=w_sb[:],
                    in_=weights[m][c * K_PASS : (c + 1) * K_PASS, :].rearrange(
                        "(p j) e -> p j e", j=PACK
                    ),
                )
                w_rows[(m, c)] = w_sb

        for m in range(1, 3):
            nc.sync.dma_start(out=bias_all[m][:], in_=biases[m].partition_broadcast(P))

        gamma_f = const.tile([P, PASSES * PACK], F32)
        beta_f = const.tile([P, PASSES * PACK], F32)

        def cast_gamma_beta():
            nc.scalar.copy(out=gamma_f[:], in_=gamma_bf[:].rearrange("p c j -> p (c j)"))
            nc.scalar.copy(out=beta_f[:], in_=beta_bf[:].rearrange("p c j -> p (c j)"))

        h_codes = [
            keep.tile([P, PASSES, ROWS], U32, name="h_codes_%d" % b, align_bytes=64)
            for b in range(BATCHES)
        ]
        h_scales = [
            keep.tile([P, PASSES, ROWS], U8, name="h_scales_%d" % b, align_bytes=64)
            for b in range(BATCHES)
        ]
        units = [(m, g * BANK_COLS, BANK_COLS) for m in range(3) for g in range(COL_GROUPS)]
        m, col, width = units.pop()
        units += [(m, col + i * TAIL_COLS, TAIL_COLS) for i in range(width // TAIL_COLS)]
        w_codes = [
            keep.tile([P, PASSES, width], U32, name="w_codes_%d" % k, align_bytes=64)
            for k, (m, col, width) in enumerate(units)
        ]
        w_scales = [
            keep.tile([P, PASSES, width], U8, name="w_scales_%d" % k, align_bytes=64)
            for k, (m, col, width) in enumerate(units)
        ]

        def quantise(codes, scales, grouped):
            nc.vector.quantize_mx(
                out=codes.bitcast(FP8X4),
                scales=scales,
                in_=grouped.rearrange("p w j -> p (w j)"),
            )


        row_tiles = [(b, i) for b in range(BATCHES) for i in range(ROW_TILES)]
        stats = const.tile([P, len(row_tiles), STATS_CHUNKS, 6], F32)
        mean_var = const.tile([P, len(row_tiles), 2], F32)
        std = const.tile([P, len(row_tiles)], F32)
        rstd = const.tile([P, len(row_tiles)], F32)
        shift = const.tile([P, len(row_tiles)], F32)
        xhat_tiles = {}
        planes = {}
        grouped_h = {}
        grouped_w = {}
        flips = {}
        sums_of = {}
        results = {}

        def bs(t, s):
            b, i = row_tiles[t]
            nc.vector.bn_stats(out=stats[:, t, s, :], in_=x_rows[b][:, i, s * STATS_CHUNK : (s + 1) * STATS_CHUNK])

        def aggr(t):
            nc.vector.bn_aggr(out=mean_var[:, t, :], in_=stats[:, t, :, :].rearrange("p s u -> p (s u)"))
            nc.scalar.activation(out=std[:, t : t + 1], in_=mean_var[:, t, 1:2], func=ACT.Sqrt, bias=eps[:, 0:1])

        sums_s = const.tile([P, len(row_tiles)], F32)
        negmean = const.tile([P, len(row_tiles)], F32)
        ssq = const.tile([P, len(row_tiles)], F32)
        junk = const.tile([P, FEATURES], BF16)

        def stats_s1(t):
            b, i = row_tiles[t]
            nc.scalar.activation(out=junk[:], in_=x_rows[b][:, i, :], func=ACT.Identity, accum_out=sums_s[:, t : t + 1])
            nc.scalar.activation(out=negmean[:, t : t + 1], in_=sums_s[:, t : t + 1], func=ACT.Copy, scale=-1.0 / FEATURES)

        def stats_s2(t):
            b, i = row_tiles[t]
            nc.scalar.activation(out=junk[:], in_=x_rows[b][:, i, :], func=ACT.Square, bias=negmean[:, t : t + 1], accum_out=ssq[:, t : t + 1])
            nc.scalar.activation(out=std[:, t : t + 1], in_=ssq[:, t : t + 1], func=ACT.Sqrt, scale=1.0 / FEATURES, bias=eps[:, 0:1])

        def small_s(t):
            nc.vector.reciprocal(out=rstd[:, t : t + 1], in_=std[:, t : t + 1])
            nc.vector.tensor_scalar(
                out=shift[:, t : t + 1], in0=negmean[:, t : t + 1], scalar1=rstd[:, t : t + 1], scalar2=1.0,
                op0=ALU.mult, op1=ALU.mult,
            )

        def small(t):
            nc.vector.reciprocal(out=rstd[:, t : t + 1], in_=std[:, t : t + 1])
            nc.vector.tensor_scalar(
                out=shift[:, t : t + 1], in0=mean_var[:, t, 0:1], scalar1=rstd[:, t : t + 1], scalar2=-1.0,
                op0=ALU.mult, op1=ALU.mult,
            )

        def xhat_of(t, eng):
            b, i = row_tiles[t]
            xhat = xhat_pool.tile([P, PASSES, PACK, P], F32, name="xhat")
            src = x_rows[b][:, i, :].rearrange("p (c q j) -> p c j q", c=PASSES, j=PACK)
            if eng == "G":
                nc.gpsimd.tensor_scalar(out=xhat[:], in0=src, scalar1=negmean[:, t : t + 1], scalar2=rstd[:, t : t + 1], op0=ALU.add, op1=ALU.mult)
            elif eng == "V":
                nc.vector.tensor_scalar(out=xhat[:], in0=src, scalar1=rstd[:, t : t + 1], scalar2=shift[:, t : t + 1], op0=ALU.mult, op1=ALU.add)
            else:
                nc.scalar.activation(out=xhat[:], in_=src, func=ACT.Identity, scale=rstd[:, t : t + 1], bias=shift[:, t : t + 1])
            xhat_tiles[(b, i)] = xhat

        def flip(b, c, j):
            if (b, c) == (0, 1):
                flipped = sum_psum.tile([P, ROW_TILES, P], F32, name="sums")
            else:
                flipped = flip_psum.tile([P, ROW_TILES, P], F32, tag="flip")
            for i in range(ROW_TILES):
                nc.tensor.transpose(flipped[:, i, :], xhat_tiles[(b, i)][:, c, j, :], ident[:])
            flips[(b, c, j)] = flipped

        def exit_h(b, c, j, eng):
            if j == 0:
                planes[(b, c)] = plane_pool.tile([P, PACK, ROWS], BF16, name="planes")
            col = c * PACK + j
            src = flips[(b, c, j)][:].rearrange("q i r -> q (i r)")
            if eng == "S":
                nc.scalar.activation(out=planes[(b, c)][:, j, :], in_=src, func=ACT.Identity, scale=gamma_f[:, col : col + 1], bias=beta_f[:, col : col + 1])
            else:
                nc.vector.tensor_scalar(out=planes[(b, c)][:, j, :], in0=src, scalar1=gamma_f[:, col : col + 1], scalar2=beta_f[:, col : col + 1], op0=ALU.mult, op1=ALU.add)

        def gp_copy(out, in_):
            nc.gpsimd.tensor_scalar(out=out, in0=in_, scalar1=1.0, scalar2=0.0, op0=ALU.mult, op1=ALU.add)

        COPY = {"V": nc.vector.tensor_copy, "S": nc.scalar.copy, "G": gp_copy}

        def hreg(b, c, eng, pieces=1):
            grouped = group_pool.tile([P, BANK_COLS, PACK], BF16, align_bytes=64, name="grouped")
            w = BANK_COLS // pieces
            for k in range(pieces):
                if eng == "G":
                    gp_copy(grouped[:, k * w : (k + 1) * w, :], planes[(b, c)][:, :, k * w : (k + 1) * w].rearrange("p j w -> p w j"))
                else:
                    regroup(COPY[eng], grouped[:, k * w : (k + 1) * w, :], planes[(b, c)][:, :, k * w : (k + 1) * w])
            grouped_h[(b, c)] = grouped

        def hquant(b, c):
            quantise(h_codes[b][:, c, :], h_scales[b][:, c, :], grouped_h[(b, c)][:])

        quarters = [(k, c) for k in range(len(units)) for c in range(PASSES)]

        def wreg(n, eng, lo=0, hi=BANK_COLS):
            k, c = quarters[n]
            m, col, width = units[k]
            lo, hi = lo * width // BANK_COLS, hi * width // BANK_COLS
            if k not in grouped_w:
                grouped_w[k] = wgroup_pool.tile([P, PASSES, width, PACK], BF16, align_bytes=64, name="wgrouped")
            rows = w_rows[(m, c)][:, :, col + lo : col + hi]
            if eng == "G":
                gp_copy(grouped_w[k][:, c, lo:hi, :], rows.rearrange("p j w -> p w j"))
            else:
                regroup(COPY[eng], grouped_w[k][:, c, lo:hi, :], rows)

        def wquant(n):
            k, c = quarters[n]
            quantise(w_codes[k][:, c, :], w_scales[k][:, c, :], grouped_w[k][:, c, :, :])

        gate_word = const.tile([P, 1], U32)

        def gate(u):
            k, c = quarters[u]
            nc.gpsimd.tensor_copy(out=gate_word[:], in_=w_codes[k][:, c, 0:1])

        products = [(k, b) for k in range(len(units)) for b in range(BATCHES)]

        def mm(n, i, c):
            k, b = products[n]
            m, col, width = units[k]
            rows = slice(i * P, (i + 1) * P)
            if c == 0:
                if n > 0 and i == 0:
                    sums = flip_psum.tile([P, width], F32, tag="flip")
                else:
                    sums = sum_psum.tile([P, width], F32, name="sums")
                sums_of[(n, i)] = sums
            nc.tensor.matmul_mx(
                out=sums_of[(n, i)][:], lhsT=h_codes[b][:, c, rows].bitcast(FP8X4), lhsT_scale=h_scales[b][:, c, rows],
                rhs=w_codes[k][:, c, :].bitcast(FP8X4), rhs_scale=w_scales[k][:, c, :],
                start=(c == 0), stop=(c == PASSES - 1),
            )

        def add(n, i, eng="V"):
            k, b = products[n]
            m, col, width = units[k]
            heads = width // HEAD_DIM
            if n not in results:
                results[n] = out_pool.tile([P, heads, ROW_TILES, HEAD_DIM], F32, name="result")
            bias_cols = bias_all[m][:, col : col + width].rearrange("p (a d) -> p a d", a=heads)
            sums = sums_of[(n, i)][:].rearrange("p (a d) -> p a d", a=heads)
            result = results[n][:, :, i, :]
            if eng == "SG":
                nc.scalar.copy(out=result, in_=sums)
                nc.gpsimd.tensor_tensor(out=result, in0=result, in1=bias_cols, op=ALU.add)
            else:
                nc.vector.tensor_tensor(out=result, in0=sums, in1=bias_cols, op=ALU.add)

        def store(n, lo, hi):
            k, b = products[n]
            m, col, width = units[k]
            first = col // HEAD_DIM
            nc.sync.dma_start(
                out=outs[m][b, first : first + width // HEAD_DIM].rearrange("a (p i) d -> p a i d", i=ROW_TILES)[:, :, lo:hi, :],
                in_=results[n][:, :, lo:hi, :],
            )

        def aggr_v(t):
            nc.vector.bn_aggr(out=mean_var[:, t, :], in_=stats[:, t, :, :].rearrange("p s u -> p (s u)"))
            nc.scalar.activation(out=std[:, t : t + 1], in_=mean_var[:, t, 1:2], func=ACT.Sqrt, bias=eps[:, 0:1])
            nc.scalar.activation(out=negmean[:, t : t + 1], in_=mean_var[:, t, 0:1], func=ACT.Copy, scale=-1.0)

        def recip(t):
            nc.vector.reciprocal(out=rstd[:, t : t + 1], in_=std[:, t : t + 1])

        def shift_v(t):
            nc.vector.tensor_scalar(
                out=shift[:, t : t + 1], in0=mean_var[:, t, 0:1], scalar1=rstd[:, t : t + 1], scalar2=-1.0,
                op0=ALU.mult, op1=ALU.mult,
            )

        def shift_s(t):
            nc.scalar.activation(out=shift[:, t : t + 1], in_=negmean[:, t : t + 1], func=ACT.Identity, scale=rstd[:, t : t + 1])

        def xhat_and_flip(t):
            xhat_of(t, "G")
            if t < ROW_TILES:
                for c in range(PASSES):
                    for j in range(PACK):
                        nc.tensor.transpose(flips[(0, c, j)][:, t, :], xhat_tiles[(0, t)][:, c, j, :], ident[:])

        def sflip():
            if ST < ROW_TILES:
                for c in range(PASSES):
                    for j in range(PACK):
                        nc.tensor.transpose(flips[(0, c, j)][:, ST, :], xhat_tiles[(0, ST)][:, c, j, :], ident[:])

        for j in range(PACK):
            flipped = flip_psum.tile([P, ROW_TILES, P], F32, tag="flip")
            flips[(0, 0, j)] = flipped
        for j in range(PACK):
            flipped = sum_psum.tile([P, ROW_TILES, P], F32, name="sums")
            flips[(0, 1, j)] = flipped
        VT = [t for t in range(8) if t != 7]
        ST = 7
        SLOT = {"s1": 0, "s2": 1, "bias": 2, "xhat": 3, "cast": 3, "q0a": 4, "q0b": 5}
        for k, t in enumerate(VT):
            bs(t, 0)
            if k >= 1:
                aggr_v(VT[k - 1])
            if k == SLOT["xhat"]:
                recip(ST)
            bs(t, 1)
            if k >= 1:
                recip(VT[k - 1])
                xhat_and_flip(VT[k - 1])
            if k == SLOT["xhat"]:
                shift_s(ST)
                xhat_of(ST, "S")
                sflip()
            if k == SLOT["s1"]:
                stats_s1(ST)
            if k == SLOT["s2"]:
                stats_s2(ST)
            if k == SLOT["cast"]:
                cast_gamma_beta()
            if k == SLOT["q0a"]:
                wreg(0, "S", 0, 256)
            if k == SLOT["q0b"]:
                wreg(0, "S", 256, 512)
        aggr_v(VT[-1])
        for j in range(4):
            exit_h(0, 0, j, "S")
        for j in range(4):
            exit_h(0, 1, j, "V")
            if j == 0:
                recip(VT[-1])
                xhat_and_flip(VT[-1])
        wreg(1, "S")
        hreg(0, 0, "V")
        wquant(0)
        hquant(0, 0)
        hreg(0, 1, "V")
        wquant(1)
        hquant(0, 1)
        for j in range(4):
            flip(1, 0, j)
            exit_h(1, 0, j, "S")
        gate(1)
        hreg(1, 0, "G", 1)
        for c in range(2):
            for i in range(4):
                mm(0, i, c)
        wreg(2, "S")
        for j in range(4):
            flip(1, 1, j)
            exit_h(1, 1, j, "S")
        for i in range(4):
            add(0, i)
        store(0, 0, 4)
        hquant(1, 0)
        for i in range(4):
            mm(1, i, 0)
        wquant(2)
        hreg(1, 1, "V")
        wreg(3, "S")
        wreg(4, "S", 0, Q4_EARLY)
        hquant(1, 1)
        for i in range(4):
            mm(1, i, 1)
        wquant(3)

        S_END = 416
        for n in range(1, len(products)):
            u = n + AHEAD
            if n > 1:
                for i in range(ROW_TILES):
                    for c in range(PASSES):
                        mm(n, i, c)
            if u < len(quarters):
                wreg(u, "G", S_END, BANK_COLS)
            add(n, 0, "SG")
            if u < len(quarters):
                wreg(u, "S", Q4_EARLY if n == 1 else 0, S_END)
            for i in range(1, ROW_TILES):
                add(n, i)
            if u < len(quarters):
                wquant(u)
            store(n, 0, ROW_TILES)
